import numpy as np
import ml_dtypes


def mxq(x, axis, fmt="e4m3"):
    dtype, down = {"e4m3": (ml_dtypes.float8_e4m3fn, 7), "e5m2": (ml_dtypes.float8_e5m2, 14)}[fmt]
    v = np.moveaxis(np.asarray(x, np.float32).astype(ml_dtypes.bfloat16).astype(np.float64), axis, -1)
    blocks = v.reshape(v.shape[:-1] + (-1, 32))
    amax = np.abs(blocks).max(-1, keepdims=True)
    byte = np.maximum(np.where(amax > 0, np.frexp(amax)[1] - 1 + 127, 0) - down, 1)
    scale = np.exp2(byte - 127.0)
    codes = (blocks / scale).astype(np.float32).astype(dtype).astype(np.float64)
    return np.moveaxis((codes * scale).reshape(v.shape), -1, axis)


WIDE = False


def mx_kscale(k):
    if not WIDE:
        return np.ones(k)
    levels = np.array([10, -10, 5, -5, 0])
    a = np.random.permutation(np.resize(levels, k // 512 * 4)).reshape(k // 512, 4)
    idx = np.arange(k)
    return np.exp2(a[idx // 512, idx % 128 // 32])


BF16 = ml_dtypes.bfloat16


def bf(x):
    return np.asarray(x, np.float32).astype(BF16)


def f64(x):
    return np.asarray(x).astype(np.float64)


N, C0, H, KS, P, C, O, F, NC = 512, 1, 4, 3, 2, 512, 512, 512, 10
KK = KS * KS
OH = H - KS + 1
OP = OH // P
FC = O * OP * OP


def relu(v):
    return np.maximum(v, 0.0)


def maxpool(v):
    n, c, hh, ww = v.shape
    hp, wp = hh // P, ww // P
    return v[:, :, :hp * P, :wp * P].reshape(n, c, hp, P, wp, P).max(axis=(3, 5))


def setup_inputs():
    s = mx_kscale(C)
    t = mx_kscale(FC)
    tt = np.repeat(np.repeat(t.reshape(O, OP, OP), P, axis=1), P, axis=2)
    h = np.maximum(np.random.standard_normal((P * P, N, C, H, H)).max(0), 0.0)
    return {
        "h_pool1": bf(h * s[None, :, None, None]),
        "w2": bf(np.random.standard_normal((O, C, KK, OH, OH)) * 0.8 / np.sqrt(KK * C) / s[None, :, None, None, None] * tt[:, None, None, :, :]),
        "b2": bf(np.random.standard_normal((O, OH, OH)) * 0.3 * tt),
        "fc1_w": bf(np.random.standard_normal((FC, F)) * 0.8 / np.sqrt(FC) / t[:, None]),
        "fc1_b": bf(np.random.standard_normal(F) * 0.3),
    }


def reference(h_pool1, w2, b2, fc1_w, fc1_b):
    hq = mxq(f64(h_pool1).transpose(2, 3, 0, 1), 3, "e4m3")
    wq = mxq(f64(w2).transpose(2, 3, 4, 1, 0), 3, "e4m3")
    y = sum((hq[i:i + OH, j:j + OH] @ wq[i * KS + j]) for i in range(KS) for j in range(KS))
    y = y.transpose(2, 3, 0, 1) + f64(b2)
    g = maxpool(relu(y)).reshape(N, FC)
    return relu((mxq(g, 1, "e4m3") @ mxq(f64(fc1_w), 0, "e4m3")) + f64(fc1_b))

@@ -1,0 +1,220 @@
+from contextlib import ExitStack
+
+import concourse.mybir as mybir
+from concourse.masks import make_identity
+
+F32 = mybir.dt.float32
+BF16 = mybir.dt.bfloat16
+U32 = mybir.dt.uint32
+U8 = mybir.dt.uint8
+FP8X4 = mybir.dt.float8_e4m3fn_x4
+ADD = mybir.AluOpType.add
+MAX = mybir.AluOpType.max
+RELU = mybir.ActivationFunctionType.Relu
+
+P = 128
+PACK = 4
+N = 512
+C = 512
+SIDE = 4
+PIXELS = SIDE * SIDE
+WINDOW = 3
+OFFSETS = WINDOW * WINDOW
+OUT_SIDE = 2
+POSITIONS = OUT_SIDE * OUT_SIDE
+TAPS = OFFSETS * POSITIONS
+O = 512
+F = 512
+N_TILES = N // P
+O_TILES = O // P
+HALF = P // 2
+
+FLOPS = 2 * N * O * C * TAPS + 2 * N * O * F
+
+
+def copy_on(nc, on_scalar, out, in_):
+    if on_scalar:
+        nc.scalar.copy(out=out, in_=in_)
+    else:
+        nc.vector.tensor_copy(out=out, in_=in_)
+
+
+def transpose_pair(nc, banks, ident, rows, inner, w):
+    words = rows.bitcast(F32).rearrange("r (p t w) -> r p t w", t=PACK, w=inner // 2)
+    bank = banks.tile([P, PACK * P], F32, tag="bank")
+    for t in range(PACK):
+        nc.tensor.transpose(bank[:, t * P : (t + 1) * P], words[:, :, t, w], ident[:])
+    return bank[:].bitcast(BF16).rearrange("p (t r e) -> p e r t", t=PACK, e=2)
+
+
+def tile_locallyconnectednet_pa_t_kernel(tc, h_pool1, w2, b2, fc1_w, fc1_b, out):
+    nc = tc.nc
+    with ExitStack() as stack:
+        keep = stack.enter_context(tc.tile_pool(name="keep", bufs=1))
+        raws = stack.enter_context(tc.tile_pool(name="raws", bufs=2))
+        weights = stack.enter_context(tc.tile_pool(name="weights", bufs=2))
+        stage = stack.enter_context(tc.tile_pool(name="stage", bufs=4))
+        work = stack.enter_context(tc.tile_pool(name="work", bufs=2))
+        banks = stack.enter_context(tc.psum_pool(name="banks", bufs=4))
+        sums = stack.enter_context(tc.psum_pool(name="sums", bufs=1))
+
+        ident = keep.tile([P, P], F32)
+        make_identity(nc, ident[:])
+
+        b2_bf = keep.tile([P, O_TILES * POSITIONS], BF16)
+        nc.scalar.dma_start(out=b2_bf[:], in_=b2.rearrange("(m t) i j -> m (t i j)", t=O_TILES))
+        b2_f32 = keep.tile([P, O_TILES * POSITIONS], F32)
+        nc.vector.tensor_copy(out=b2_f32[:], in_=b2_bf[:])
+
+        h_codes = keep.tile([P, PIXELS, N], U32, align_bytes=64)
+        h_scales = keep.tile([P, PIXELS, N], U8, align_bytes=64)
+
+        def load_images(pair):
+            raw = raws.tile([P, C * TAPS], BF16, tag="raw")
+            for half in range(2):
+                nt = 2 * pair + half
+                nc.sync.dma_start(
+                    out=raw[:, half * C * PIXELS : (half + 1) * C * PIXELS],
+                    in_=h_pool1[nt * P : (nt + 1) * P].rearrange("n c y x -> n (c y x)"),
+                )
+            return raw
+
+        def quantise_images(pair, raw):
+            for half in range(2):
+                nt = 2 * pair + half
+                rows = raw[:, half * C * PIXELS : (half + 1) * C * PIXELS]
+                for w in range(PIXELS // 2):
+                    bank = transpose_pair(nc, banks, ident, rows, PIXELS, w)
+                    h_grouped = stage.tile([P, 2, P, PACK], BF16, align_bytes=64)
+                    copy_on(nc, w % 3 != 2, h_grouped[:], bank)
+                    for e in range(2):
+                        nc.vector.quantize_mx(
+                            out=h_codes[:, 2 * w + e, nt * P : (nt + 1) * P].bitcast(FP8X4),
+                            scales=h_scales[:, 2 * w + e, nt * P : (nt + 1) * P],
+                            in_=h_grouped[:, e].rearrange("p r t -> p (r t)"),
+                        )
+
+        def load_weights(t):
+            raw = raws.tile([P, C * TAPS], BF16, tag="raw")
+            if t % 2 == 0:
+                nc.sync.dma_start(
+                    out=raw[:],
+                    in_=w2.rearrange("(m t) c k i j -> t m (c k i j)", t=O_TILES)[t],
+                )
+            else:
+                source = w2.rearrange("(m t) (p c) k i j -> t p m (c k i j)", t=O_TILES, c=PACK)[t]
+                target = raw[:].rearrange("p (m x) -> p m x", m=P)
+                for m0 in range(0, P, HALF):
+                    nc.sync.dma_start(
+                        out=target[:, m0 : m0 + HALF, :], in_=source[:, m0 : m0 + HALF, :]
+                    )
+            return raw
+
+        def quantise_weights(t, raw):
+            w_codes = weights.tile([P, OFFSETS, POSITIONS * P], U32, align_bytes=64)
+            w_scales = weights.tile([P, OFFSETS, POSITIONS * P], U8, align_bytes=64)
+            for k in range(OFFSETS):
+                w_grouped = stage.tile([P, POSITIONS, P, PACK], BF16, align_bytes=64)
+                if t % 2 == 0:
+                    for half in range(2):
+                        w = 2 * k + half
+                        bank = transpose_pair(nc, banks, ident, raw[:], TAPS, w)
+                        copy_on(nc, w % 3 != 2, w_grouped[:, 2 * half : 2 * half + 2], bank)
+                else:
+                    taps = raw[:].rearrange("p (m c q) -> p m c q", c=PACK, q=TAPS)
+                    for m0 in range(0, P, HALF):
+                        copy_on(
+                            nc,
+                            k % 2 == 0,
+                            w_grouped[:, :, m0 : m0 + HALF, :].rearrange("p i m c -> p m c i"),
+                            taps[:, m0 : m0 + HALF, :, k * POSITIONS : (k + 1) * POSITIONS],
+                        )
+                nc.vector.quantize_mx(
+                    out=w_codes[:, k, :].bitcast(FP8X4),
+                    scales=w_scales[:, k, :],
+                    in_=w_grouped[:].rearrange("p i m c -> p (i m c)"),
+                )
+            return w_codes, w_scales
+
+        g_grouped = keep.tile([P, N, PACK], BF16, align_bytes=64)
+
+        def convolve_and_pool(t, w_codes, w_scales):
+            acc = [sums.tile([P, N], F32, name="acc%d" % pos) for pos in range(POSITIONS)]
+            for k in range(OFFSETS):
+                for pos in range(POSITIONS):
+                    pixel = (pos // OUT_SIDE + k // WINDOW) * SIDE + pos % OUT_SIDE + k % WINDOW
+                    nc.tensor.matmul_mx(
+                        out=acc[pos][:],
+                        lhsT=w_codes[:, k, pos * P : (pos + 1) * P].bitcast(FP8X4),
+                        lhsT_scale=w_scales[:, k, pos * P : (pos + 1) * P],
+                        rhs=h_codes[:, pixel, :].bitcast(FP8X4),
+                        rhs_scale=h_scales[:, pixel, :],
+                        start=(k == 0),
+                        stop=(k == OFFSETS - 1),
+                    )
+            best = work.tile([P, N], F32)
+            nc.scalar.activation(
+                out=best[:], in_=acc[0][:], func=RELU, bias=b2_f32[:, t * POSITIONS : t * POSITIONS + 1]
+            )
+            for pos in range(1, POSITIONS):
+                last = pos == POSITIONS - 1
+                nc.vector.scalar_tensor_tensor(
+                    out=g_grouped[:, :, t] if last else best[:],
+                    in0=acc[pos][:],
+                    scalar=b2_f32[:, t * POSITIONS + pos : t * POSITIONS + pos + 1],
+                    in1=best[:],
+                    op0=ADD,
+                    op1=MAX,
+                )
+
+        raw_images = [load_images(0), load_images(1)]
+        raw_weights = {}
+        quantise_images(0, raw_images[0])
+        raw_weights[0] = load_weights(0)
+        quantise_images(1, raw_images[1])
+        raw_weights[1] = load_weights(1)
+
+        fc_raw = keep.tile([P, PACK, F], BF16)
+        nc.sync.dma_start(out=fc_raw[:], in_=fc1_w.rearrange("(m t) f -> m t f", t=PACK))
+        fc_grouped = keep.tile([P, F, PACK], BF16, align_bytes=64)
+        fc_codes = keep.tile([P, F], U32, align_bytes=64)
+        fc_scales = keep.tile([P, F], U8, align_bytes=64)
+        bias = keep.tile([P, F], BF16)
+
+        for t in range(O_TILES):
+            w_codes, w_scales = quantise_weights(t, raw_weights[t])
+            if t + 2 < O_TILES:
+                raw_weights[t + 2] = load_weights(t + 2)
+            convolve_and_pool(t, w_codes, w_scales)
+            if t == 0:
+                nc.vector.tensor_copy(out=fc_grouped[:], in_=fc_raw[:].rearrange("p t f -> p f t"))
+                nc.vector.quantize_mx(
+                    out=fc_codes[:].bitcast(FP8X4),
+                    scales=fc_scales[:],
+                    in_=fc_grouped[:].rearrange("p f t -> p (f t)"),
+                )
+        nc.sync.dma_start(out=bias[:], in_=fc1_b.partition_broadcast(P))
+
+        g_codes = keep.tile([P, N], U32, align_bytes=64)
+        g_scales = keep.tile([P, N], U8, align_bytes=64)
+        nc.vector.quantize_mx(
+            out=g_codes[:].bitcast(FP8X4),
+            scales=g_scales[:],
+            in_=g_grouped[:].rearrange("p n t -> p (n t)"),
+        )
+        for nt in range(N_TILES):
+            dense = sums.tile([P, F], F32, name="acc%d" % nt)
+            nc.tensor.matmul_mx(
+                out=dense[:],
+                lhsT=g_codes[:, nt * P : (nt + 1) * P].bitcast(FP8X4),
+                lhsT_scale=g_scales[:, nt * P : (nt + 1) * P],
+                rhs=fc_codes[:].bitcast(FP8X4),
+                rhs_scale=fc_scales[:],
+                start=True,
+                stop=True,
+            )
+            summed = work.tile([P, F], F32)
+            nc.vector.tensor_tensor(out=summed[:], in0=dense[:], in1=bias[:], op=ADD)
+            result = work.tile([P, F], F32)
+            nc.scalar.activation(out=result[:], in_=summed[:], func=RELU)
+            nc.sync.dma_start(out=out[nt * P : (nt + 1) * P, :], in_=result[:])

@@ -27,9 +27,10 @@ O = 512
 F = 512
 N_TILES = N // P
 O_TILES = O // P
-HALF = P // 2
 
 FLOPS = 2 * N * O * C * TAPS + 2 * N * O * F
+
+RUN = 2
 
 
 def copy_on(nc, on_scalar, out, in_):
@@ -50,24 +51,15 @@ def transpose_pair(nc, banks, ident, rows, inner, w):
 def tile_locallyconnectednet_pa_t_kernel(tc, h_pool1, w2, b2, fc1_w, fc1_b, out):
     nc = tc.nc
     with ExitStack() as stack:
+        stack.enter_context(tc.manual_schedule())
         keep = stack.enter_context(tc.tile_pool(name="keep", bufs=1))
         raws = stack.enter_context(tc.tile_pool(name="raws", bufs=2))
         weights = stack.enter_context(tc.tile_pool(name="weights", bufs=2))
         stage = stack.enter_context(tc.tile_pool(name="stage", bufs=4))
+        w_stage = stack.enter_context(tc.tile_pool(name="w_stage", bufs=3 * RUN))
         work = stack.enter_context(tc.tile_pool(name="work", bufs=2))
         banks = stack.enter_context(tc.psum_pool(name="banks", bufs=4))
         sums = stack.enter_context(tc.psum_pool(name="sums", bufs=1))
-
-        ident = keep.tile([P, P], F32)
-        make_identity(nc, ident[:])
-
-        b2_bf = keep.tile([P, O_TILES * POSITIONS], BF16)
-        nc.scalar.dma_start(out=b2_bf[:], in_=b2.rearrange("(m t) i j -> m (t i j)", t=O_TILES))
-        b2_f32 = keep.tile([P, O_TILES * POSITIONS], F32)
-        nc.vector.tensor_copy(out=b2_f32[:], in_=b2_bf[:])
-
-        h_codes = keep.tile([P, PIXELS, N], U32, align_bytes=64)
-        h_scales = keep.tile([P, PIXELS, N], U8, align_bytes=64)
 
         def load_images(pair):
             raw = raws.tile([P, C * TAPS], BF16, tag="raw")
@@ -79,122 +71,160 @@ def tile_locallyconnectednet_pa_t_kernel(tc, h_pool1, w2, b2, fc1_w, fc1_b, out)
                 )
             return raw
 
-        def quantise_images(pair, raw):
-            for half in range(2):
-                nt = 2 * pair + half
-                rows = raw[:, half * C * PIXELS : (half + 1) * C * PIXELS]
-                for w in range(PIXELS // 2):
-                    bank = transpose_pair(nc, banks, ident, rows, PIXELS, w)
-                    h_grouped = stage.tile([P, 2, P, PACK], BF16, align_bytes=64)
-                    copy_on(nc, w % 3 != 2, h_grouped[:], bank)
-                    for e in range(2):
-                        nc.vector.quantize_mx(
-                            out=h_codes[:, 2 * w + e, nt * P : (nt + 1) * P].bitcast(FP8X4),
-                            scales=h_scales[:, 2 * w + e, nt * P : (nt + 1) * P],
-                            in_=h_grouped[:, e].rearrange("p r t -> p (r t)"),
-                        )
+        def by_transposes(t):
+            return t % 2 == 0
 
         def load_weights(t):
             raw = raws.tile([P, C * TAPS], BF16, tag="raw")
-            if t % 2 == 0:
-                nc.sync.dma_start(
-                    out=raw[:],
-                    in_=w2.rearrange("(m t) c k i j -> t m (c k i j)", t=O_TILES)[t],
-                )
+            if by_transposes(t):
+                source = w2.rearrange("(m t) c k i j -> t m (c k i j)", t=O_TILES)[t]
+                cut = C * TAPS // 2
+                for x0 in (0, cut):
+                    nc.sync.dma_start(out=raw[:, x0 : x0 + cut], in_=source[:, x0 : x0 + cut])
             else:
                 source = w2.rearrange("(m t) (p c) k i j -> t p m (c k i j)", t=O_TILES, c=PACK)[t]
                 target = raw[:].rearrange("p (m x) -> p m x", m=P)
-                for m0 in range(0, P, HALF):
-                    nc.sync.dma_start(
-                        out=target[:, m0 : m0 + HALF, :], in_=source[:, m0 : m0 + HALF, :]
-                    )
+                cut = P // 2
+                for m0 in (0, cut):
+                    nc.sync.dma_start(out=target[:, m0 : m0 + cut, :], in_=source[:, m0 : m0 + cut, :])
             return raw
-
-        def quantise_weights(t, raw):
-            w_codes = weights.tile([P, OFFSETS, POSITIONS * P], U32, align_bytes=64)
-            w_scales = weights.tile([P, OFFSETS, POSITIONS * P], U8, align_bytes=64)
-            for k in range(OFFSETS):
-                w_grouped = stage.tile([P, POSITIONS, P, PACK], BF16, align_bytes=64)
-                if t % 2 == 0:
-                    for half in range(2):
-                        w = 2 * k + half
-                        bank = transpose_pair(nc, banks, ident, raw[:], TAPS, w)
-                        copy_on(nc, w % 3 != 2, w_grouped[:, 2 * half : 2 * half + 2], bank)
-                else:
-                    taps = raw[:].rearrange("p (m c q) -> p m c q", c=PACK, q=TAPS)
-                    for m0 in range(0, P, HALF):
-                        copy_on(
-                            nc,
-                            k % 2 == 0,
-                            w_grouped[:, :, m0 : m0 + HALF, :].rearrange("p i m c -> p m c i"),
-                            taps[:, m0 : m0 + HALF, :, k * POSITIONS : (k + 1) * POSITIONS],
-                        )
-                nc.vector.quantize_mx(
-                    out=w_codes[:, k, :].bitcast(FP8X4),
-                    scales=w_scales[:, k, :],
-                    in_=w_grouped[:].rearrange("p i m c -> p (i m c)"),
-                )
-            return w_codes, w_scales
-
-        g_grouped = keep.tile([P, N, PACK], BF16, align_bytes=64)
-
-        def convolve_and_pool(t, w_codes, w_scales):
-            acc = [sums.tile([P, N], F32, name="acc%d" % pos) for pos in range(POSITIONS)]
-            for k in range(OFFSETS):
-                for pos in range(POSITIONS):
-                    pixel = (pos // OUT_SIDE + k // WINDOW) * SIDE + pos % OUT_SIDE + k % WINDOW
-                    nc.tensor.matmul_mx(
-                        out=acc[pos][:],
-                        lhsT=w_codes[:, k, pos * P : (pos + 1) * P].bitcast(FP8X4),
-                        lhsT_scale=w_scales[:, k, pos * P : (pos + 1) * P],
-                        rhs=h_codes[:, pixel, :].bitcast(FP8X4),
-                        rhs_scale=h_scales[:, pixel, :],
-                        start=(k == 0),
-                        stop=(k == OFFSETS - 1),
-                    )
-            best = work.tile([P, N], F32)
-            nc.scalar.activation(
-                out=best[:], in_=acc[0][:], func=RELU, bias=b2_f32[:, t * POSITIONS : t * POSITIONS + 1]
-            )
-            for pos in range(1, POSITIONS):
-                last = pos == POSITIONS - 1
-                nc.vector.scalar_tensor_tensor(
-                    out=g_grouped[:, :, t] if last else best[:],
-                    in0=acc[pos][:],
-                    scalar=b2_f32[:, t * POSITIONS + pos : t * POSITIONS + pos + 1],
-                    in1=best[:],
-                    op0=ADD,
-                    op1=MAX,
-                )
 
         raw_images = [load_images(0), load_images(1)]
         raw_weights = {}
-        quantise_images(0, raw_images[0])
-        raw_weights[0] = load_weights(0)
-        quantise_images(1, raw_images[1])
-        raw_weights[1] = load_weights(1)
+
+        ident = keep.tile([P, P], F32)
+        make_identity(nc, ident[:])
+
+        b2_bf = keep.tile([P, O_TILES * POSITIONS], BF16)
+        nc.scalar.dma_start(out=b2_bf[:], in_=b2.rearrange("(m t) i j -> m (t i j)", t=O_TILES))
+        b2_f32 = keep.tile([P, O_TILES * POSITIONS], F32)
+        nc.vector.tensor_copy(out=b2_f32[:], in_=b2_bf[:])
+
+        h_codes = keep.tile([P, PIXELS, N], U32, align_bytes=64)
+        h_scales = keep.tile([P, PIXELS, N], U8, align_bytes=64)
+        h_grouped = {}
+
+        def group_images(nt, w):
+            rows = raw_images[nt // 2][:, (nt % 2) * C * PIXELS : (nt % 2 + 1) * C * PIXELS]
+            bank = transpose_pair(nc, banks, ident, rows, PIXELS, w)
+            h_grouped[nt, w] = stage.tile([P, 2, P, PACK], BF16, align_bytes=64, name="h_grouped")
+            copy_on(nc, w % 3 != 2, h_grouped[nt, w][:], bank)
+
+        def quantise_images(nt, w):
+            for e in range(2):
+                nc.vector.quantize_mx(
+                    out=h_codes[:, 2 * w + e, nt * P : (nt + 1) * P].bitcast(FP8X4),
+                    scales=h_scales[:, 2 * w + e, nt * P : (nt + 1) * P],
+                    in_=h_grouped[nt, w][:, e].rearrange("p r t -> p (r t)"),
+                )
+
+        image_units = [(nt, w) for nt in range(N_TILES) for w in range(PIXELS // 2)]
+        for step in range(len(image_units) + 1):
+            if step < len(image_units):
+                group_images(*image_units[step])
+                if (step + 1) % (2 * PIXELS // 2) == 0:
+                    pair = step // (2 * PIXELS // 2)
+                    raw_weights[pair] = load_weights(pair)
+            if step >= 1:
+                quantise_images(*image_units[step - 1])
 
         fc_raw = keep.tile([P, PACK, F], BF16)
         nc.sync.dma_start(out=fc_raw[:], in_=fc1_w.rearrange("(m t) f -> m t f", t=PACK))
         fc_grouped = keep.tile([P, F, PACK], BF16, align_bytes=64)
         fc_codes = keep.tile([P, F], U32, align_bytes=64)
         fc_scales = keep.tile([P, F], U8, align_bytes=64)
-        bias = keep.tile([P, F], BF16)
 
-        for t in range(O_TILES):
-            w_codes, w_scales = quantise_weights(t, raw_weights[t])
-            if t + 2 < O_TILES:
-                raw_weights[t + 2] = load_weights(t + 2)
-            convolve_and_pool(t, w_codes, w_scales)
-            if t == 0:
+        w_grouped = {}
+        w_codes = {}
+        w_scales = {}
+        acc = {}
+        g_grouped = keep.tile([P, N, PACK], BF16, align_bytes=64)
+
+        def group_weights(t, k):
+            grouped = w_stage.tile([P, POSITIONS, P, PACK], BF16, align_bytes=64, name="w_grouped")
+            w_grouped[t, k] = grouped
+            if by_transposes(t):
+                for half in range(2):
+                    w = 2 * k + half
+                    bank = transpose_pair(nc, banks, ident, raw_weights[t][:], TAPS, w)
+                    copy_on(nc, w % 3 != 2, grouped[:, 2 * half : 2 * half + 2], bank)
+            else:
+                taps = raw_weights[t][:].rearrange("p (m c q) -> p m c q", c=PACK, q=TAPS)
+                copy_on(
+                    nc,
+                    k % 2 == 0,
+                    grouped[:].rearrange("p i m c -> p m c i"),
+                    taps[:, :, :, k * POSITIONS : (k + 1) * POSITIONS],
+                )
+
+        def quantise_weights(t, k):
+            if k == 0:
+                w_codes[t] = weights.tile([P, OFFSETS, POSITIONS * P], U32, align_bytes=64, name="w_codes")
+                w_scales[t] = weights.tile([P, OFFSETS, POSITIONS * P], U8, align_bytes=64, name="w_scales")
+            nc.vector.quantize_mx(
+                out=w_codes[t][:, k, :].bitcast(FP8X4),
+                scales=w_scales[t][:, k, :],
+                in_=w_grouped[t, k][:].rearrange("p i m c -> p (i m c)"),
+            )
+
+        def multiply(t, k):
+            for pos in range(POSITIONS):
+                if k == 0:
+                    acc[pos] = sums.tile([P, N], F32, name="acc%d" % pos)
+                pixel = (pos // OUT_SIDE + k // WINDOW) * SIDE + pos % OUT_SIDE + k % WINDOW
+                nc.tensor.matmul_mx(
+                    out=acc[pos][:],
+                    lhsT=w_codes[t][:, k, pos * P : (pos + 1) * P].bitcast(FP8X4),
+                    lhsT_scale=w_scales[t][:, k, pos * P : (pos + 1) * P],
+                    rhs=h_codes[:, pixel, :].bitcast(FP8X4),
+                    rhs_scale=h_scales[:, pixel, :],
+                    start=(k == 0),
+                    stop=(k == OFFSETS - 1),
+                )
+
+        def pool_positions(t):
+            def b2_column(pos):
+                return b2_f32[:, t * POSITIONS + pos : t * POSITIONS + pos + 1]
+
+            even = work.tile([P, 2, N], F32)
+            odd = work.tile([P, N], F32)
+            nc.scalar.activation(out=even[:, 0, :], in_=acc[0][:], func=RELU, bias=b2_column(0))
+            nc.vector.tensor_scalar(
+                out=odd[:], in0=acc[1][:], scalar1=b2_column(1), scalar2=None, op0=ADD
+            )
+            nc.scalar.activation(out=even[:, 1, :], in_=acc[2][:], func=RELU, bias=b2_column(2))
+            nc.vector.scalar_tensor_tensor(
+                out=odd[:], in0=acc[3][:], scalar=b2_column(3), in1=odd[:], op0=ADD, op1=MAX
+            )
+            nc.vector.tensor_tensor(out=odd[:], in0=odd[:], in1=even[:, 0, :], op=MAX)
+            nc.vector.tensor_tensor(out=g_grouped[:, :, t], in0=odd[:], in1=even[:, 1, :], op=MAX)
+
+        weight_units = [(t, k) for t in range(O_TILES) for k in range(OFFSETS)]
+        rounds = [weight_units[u : u + RUN] for u in range(0, len(weight_units), RUN)]
+        for r in range(len(rounds) + 2):
+            if r < len(rounds):
+                for t, k in rounds[r]:
+                    group_weights(t, k)
+                    if k == OFFSETS - 1 and t + 2 < O_TILES:
+                        raw_weights[t + 2] = load_weights(t + 2)
+            if 1 <= r <= len(rounds):
+                for t, k in rounds[r - 1]:
+                    quantise_weights(t, k)
+            if r >= 2:
+                for t, k in rounds[r - 2]:
+                    multiply(t, k)
+                    if k == OFFSETS - 1:
+                        pool_positions(t)
+            if r == len(rounds) // 2:
                 nc.vector.tensor_copy(out=fc_grouped[:], in_=fc_raw[:].rearrange("p t f -> p f t"))
                 nc.vector.quantize_mx(
                     out=fc_codes[:].bitcast(FP8X4),
                     scales=fc_scales[:],
                     in_=fc_grouped[:].rearrange("p f t -> p (f t)"),
                 )
-        nc.sync.dma_start(out=bias[:], in_=fc1_b.partition_broadcast(P))
 
+        bias = keep.tile([P, F], BF16)
+        nc.sync.dma_start(out=bias[:], in_=fc1_b.partition_broadcast(P))
         g_codes = keep.tile([P, N], U32, align_bytes=64)
         g_scales = keep.tile([P, N], U8, align_bytes=64)
         nc.vector.quantize_mx(

@@ -33,6 +33,10 @@ FLOPS = 2 * N * O * C * TAPS + 2 * N * O * F
 RUN = 2
 
 
+def to_scalar(bank_number):
+    return bank_number % 3 != 2
+
+
 def copy_on(nc, on_scalar, out, in_):
     if on_scalar:
         nc.scalar.copy(out=out, in_=in_)
@@ -108,7 +112,7 @@ def tile_locallyconnectednet_pa_t_kernel(tc, h_pool1, w2, b2, fc1_w, fc1_b, out)
             rows = raw_images[nt // 2][:, (nt % 2) * C * PIXELS : (nt % 2 + 1) * C * PIXELS]
             bank = transpose_pair(nc, banks, ident, rows, PIXELS, w)
             h_grouped[nt, w] = stage.tile([P, 2, P, PACK], BF16, align_bytes=64, name="h_grouped")
-            copy_on(nc, w % 3 != 2, h_grouped[nt, w][:], bank)
+            copy_on(nc, to_scalar(nt * (PIXELS // 2) + w), h_grouped[nt, w][:], bank)
 
         def quantise_images(nt, w):
             for e in range(2):
@@ -147,15 +151,17 @@ def tile_locallyconnectednet_pa_t_kernel(tc, h_pool1, w2, b2, fc1_w, fc1_b, out)
                 for half in range(2):
                     w = 2 * k + half
                     bank = transpose_pair(nc, banks, ident, raw_weights[t][:], TAPS, w)
-                    copy_on(nc, w % 3 != 2, grouped[:, 2 * half : 2 * half + 2], bank)
+                    copy_on(nc, to_scalar(w), grouped[:, 2 * half : 2 * half + 2], bank)
             else:
                 taps = raw_weights[t][:].rearrange("p (m c q) -> p m c q", c=PACK, q=TAPS)
-                copy_on(
-                    nc,
-                    k % 2 == 0,
-                    grouped[:].rearrange("p i m c -> p m c i"),
-                    taps[:, :, :, k * POSITIONS : (k + 1) * POSITIONS],
-                )
+                cut = P // 2
+                for m0 in (0, cut):
+                    copy_on(
+                        nc,
+                        k % 2 == 0,
+                        grouped[:, :, m0 : m0 + cut, :].rearrange("p i m c -> p m c i"),
+                        taps[:, m0 : m0 + cut, :, k * POSITIONS : (k + 1) * POSITIONS],
+                    )
 
         def quantise_weights(t, k):
             if k == 0:

@@ -27,14 +27,11 @@ O = 512
 F = 512
 N_TILES = N // P
 O_TILES = O // P
+HALF = P // 2
 
 FLOPS = 2 * N * O * C * TAPS + 2 * N * O * F
 
-RUN = 2
-
-
-def to_scalar(bank_number):
-    return bank_number % 3 != 2
+EARLY_FROM = 4
 
 
 def copy_on(nc, on_scalar, out, in_):
@@ -57,16 +54,18 @@ def tile_locallyconnectednet_pa_t_kernel(tc, h_pool1, w2, b2, fc1_w, fc1_b, out)
     with ExitStack() as stack:
         stack.enter_context(tc.manual_schedule())
         keep = stack.enter_context(tc.tile_pool(name="keep", bufs=1))
-        raws = stack.enter_context(tc.tile_pool(name="raws", bufs=2))
-        weights = stack.enter_context(tc.tile_pool(name="weights", bufs=2))
+        raws = stack.enter_context(tc.tile_pool(name="raws", bufs=3))
+        codes = stack.enter_context(tc.tile_pool(name="codes", bufs=6))
         stage = stack.enter_context(tc.tile_pool(name="stage", bufs=4))
-        w_stage = stack.enter_context(tc.tile_pool(name="w_stage", bufs=3 * RUN))
         work = stack.enter_context(tc.tile_pool(name="work", bufs=2))
         banks = stack.enter_context(tc.psum_pool(name="banks", bufs=4))
         sums = stack.enter_context(tc.psum_pool(name="sums", bufs=1))
 
+        def raw_tile():
+            return raws.tile([P, C * TAPS], BF16, tag="raw", align_bytes=64, name="raw")
+
         def load_images(pair):
-            raw = raws.tile([P, C * TAPS], BF16, tag="raw")
+            raw = raw_tile()
             for half in range(2):
                 nt = 2 * pair + half
                 nc.sync.dma_start(
@@ -79,7 +78,7 @@ def tile_locallyconnectednet_pa_t_kernel(tc, h_pool1, w2, b2, fc1_w, fc1_b, out)
             return t % 2 == 0
 
         def load_weights(t):
-            raw = raws.tile([P, C * TAPS], BF16, tag="raw")
+            raw = raw_tile()
             if by_transposes(t):
                 source = w2.rearrange("(m t) c k i j -> t m (c k i j)", t=O_TILES)[t]
                 cut = C * TAPS // 2
@@ -88,13 +87,12 @@ def tile_locallyconnectednet_pa_t_kernel(tc, h_pool1, w2, b2, fc1_w, fc1_b, out)
             else:
                 source = w2.rearrange("(m t) (p c) k i j -> t p m (c k i j)", t=O_TILES, c=PACK)[t]
                 target = raw[:].rearrange("p (m x) -> p m x", m=P)
-                cut = P // 2
-                for m0 in (0, cut):
-                    nc.sync.dma_start(out=target[:, m0 : m0 + cut, :], in_=source[:, m0 : m0 + cut, :])
+                for m0 in (0, HALF):
+                    nc.sync.dma_start(out=target[:, m0 : m0 + HALF, :], in_=source[:, m0 : m0 + HALF, :])
             return raw
 
         raw_images = [load_images(0), load_images(1)]
-        raw_weights = {}
+        raw_weights = {0: load_weights(0)}
 
         ident = keep.tile([P, P], F32)
         make_identity(nc, ident[:])
@@ -111,8 +109,8 @@ def tile_locallyconnectednet_pa_t_kernel(tc, h_pool1, w2, b2, fc1_w, fc1_b, out)
         def group_images(nt, w):
             rows = raw_images[nt // 2][:, (nt % 2) * C * PIXELS : (nt % 2 + 1) * C * PIXELS]
             bank = transpose_pair(nc, banks, ident, rows, PIXELS, w)
-            h_grouped[nt, w] = stage.tile([P, 2, P, PACK], BF16, align_bytes=64, name="h_grouped")
-            copy_on(nc, to_scalar(nt * (PIXELS // 2) + w), h_grouped[nt, w][:], bank)
+            h_grouped[nt, w] = stage.tile([P, 2, P, PACK], BF16, align_bytes=64, tag="grouped", name="h_grouped")
+            copy_on(nc, (nt * (PIXELS // 2) + w) % 3 != 2, h_grouped[nt, w][:], bank)
 
         def quantise_images(nt, w):
             for e in range(2):
@@ -128,109 +126,124 @@ def tile_locallyconnectednet_pa_t_kernel(tc, h_pool1, w2, b2, fc1_w, fc1_b, out)
                 group_images(*image_units[step])
                 if (step + 1) % (2 * PIXELS // 2) == 0:
                     pair = step // (2 * PIXELS // 2)
-                    raw_weights[pair] = load_weights(pair)
+                    raw_weights[pair + 1] = load_weights(pair + 1)
             if step >= 1:
                 quantise_images(*image_units[step - 1])
 
-        fc_raw = keep.tile([P, PACK, F], BF16)
-        nc.sync.dma_start(out=fc_raw[:], in_=fc1_w.rearrange("(m t) f -> m t f", t=PACK))
-        fc_grouped = keep.tile([P, F, PACK], BF16, align_bytes=64)
-        fc_codes = keep.tile([P, F], U32, align_bytes=64)
-        fc_scales = keep.tile([P, F], U8, align_bytes=64)
-
+        late_stage = keep.tile([P, OFFSETS, POSITIONS, P, PACK], BF16, align_bytes=64)
+        bank_views = {}
         w_grouped = {}
         w_codes = {}
         w_scales = {}
         acc = {}
+        pooled = {}
         g_grouped = keep.tile([P, N, PACK], BF16, align_bytes=64)
 
-        def group_weights(t, k):
-            grouped = w_stage.tile([P, POSITIONS, P, PACK], BF16, align_bytes=64, name="w_grouped")
-            w_grouped[t, k] = grouped
-            if by_transposes(t):
-                for half in range(2):
-                    w = 2 * k + half
-                    bank = transpose_pair(nc, banks, ident, raw_weights[t][:], TAPS, w)
-                    copy_on(nc, to_scalar(w), grouped[:, 2 * half : 2 * half + 2], bank)
-            else:
-                taps = raw_weights[t][:].rearrange("p (m c q) -> p m c q", c=PACK, q=TAPS)
-                cut = P // 2
-                for m0 in (0, cut):
-                    copy_on(
-                        nc,
-                        k % 2 == 0,
-                        grouped[:, :, m0 : m0 + cut, :].rearrange("p i m c -> p m c i"),
-                        taps[:, m0 : m0 + cut, :, k * POSITIONS : (k + 1) * POSITIONS],
-                    )
+        def transposes(t, k):
+            bank_views[t, k] = [
+                transpose_pair(nc, banks, ident, raw_weights[t][:], TAPS, 2 * k + half) for half in range(2)
+            ]
+
+        def copy_banks(t, k):
+            grouped = stage.tile([P, POSITIONS, P, PACK], BF16, align_bytes=64, tag="grouped", name="w_grouped")
+            w_grouped[t, k] = grouped[:].rearrange("p i m c -> p (i m c)")
+            copy_on(nc, True, grouped[:, 0:2], bank_views[t, k][0])
+            copy_on(nc, k >= EARLY_FROM, grouped[:, 2:4], bank_views[t, k][1])
+
+        def regroup_half(t, k, m0, on_scalar):
+            taps = raw_weights[t][:].rearrange("p (m c q) -> p m c q", c=PACK, q=TAPS)
+            copy_on(
+                nc,
+                on_scalar,
+                late_stage[:, k, :, m0 : m0 + HALF, :].rearrange("p i m c -> p m c i"),
+                taps[:, m0 : m0 + HALF, :, k * POSITIONS : (k + 1) * POSITIONS],
+            )
 
         def quantise_weights(t, k):
+            if not by_transposes(t):
+                w_grouped[t, k] = late_stage[:, k].rearrange("p i m c -> p (i m c)")
+            w_codes[t, k] = codes.tile([P, POSITIONS * P], U32, align_bytes=64, name="w_codes")
+            w_scales[t, k] = codes.tile([P, POSITIONS * P], U8, align_bytes=64, name="w_scales")
+            nc.vector.quantize_mx(out=w_codes[t, k][:].bitcast(FP8X4), scales=w_scales[t, k][:], in_=w_grouped[t, k])
+
+        def multiply(t, k, pos):
             if k == 0:
-                w_codes[t] = weights.tile([P, OFFSETS, POSITIONS * P], U32, align_bytes=64, name="w_codes")
-                w_scales[t] = weights.tile([P, OFFSETS, POSITIONS * P], U8, align_bytes=64, name="w_scales")
-            nc.vector.quantize_mx(
-                out=w_codes[t][:, k, :].bitcast(FP8X4),
-                scales=w_scales[t][:, k, :],
-                in_=w_grouped[t, k][:].rearrange("p i m c -> p (i m c)"),
+                acc[pos] = sums.tile([P, N], F32, name="acc%d" % pos)
+            pixel = (pos // OUT_SIDE + k // WINDOW) * SIDE + pos % OUT_SIDE + k % WINDOW
+            nc.tensor.matmul_mx(
+                out=acc[pos][:],
+                lhsT=w_codes[t, k][:, pos * P : (pos + 1) * P].bitcast(FP8X4),
+                lhsT_scale=w_scales[t, k][:, pos * P : (pos + 1) * P],
+                rhs=h_codes[:, pixel, :].bitcast(FP8X4),
+                rhs_scale=h_scales[:, pixel, :],
+                start=(k == 0),
+                stop=(k == OFFSETS - 1),
             )
 
-        def multiply(t, k):
-            for pos in range(POSITIONS):
-                if k == 0:
-                    acc[pos] = sums.tile([P, N], F32, name="acc%d" % pos)
-                pixel = (pos // OUT_SIDE + k // WINDOW) * SIDE + pos % OUT_SIDE + k % WINDOW
-                nc.tensor.matmul_mx(
-                    out=acc[pos][:],
-                    lhsT=w_codes[t][:, k, pos * P : (pos + 1) * P].bitcast(FP8X4),
-                    lhsT_scale=w_scales[t][:, k, pos * P : (pos + 1) * P],
-                    rhs=h_codes[:, pixel, :].bitcast(FP8X4),
-                    rhs_scale=h_scales[:, pixel, :],
-                    start=(k == 0),
-                    stop=(k == OFFSETS - 1),
+        def pool_position(t, pos):
+            bias_column = b2_f32[:, t * POSITIONS + pos : t * POSITIONS + pos + 1]
+            if pos == 0:
+                pooled[t] = work.tile([P, N], F32, tag="pooled", name="pooled")
+                nc.scalar.activation(out=pooled[t][:], in_=acc[0][:], func=RELU, bias=bias_column)
+            else:
+                target = g_grouped[:, :, t] if pos == POSITIONS - 1 else pooled[t][:]
+                nc.vector.scalar_tensor_tensor(
+                    out=target, in0=acc[pos][:], scalar=bias_column, in1=pooled[t][:], op0=ADD, op1=MAX
                 )
 
-        def pool_positions(t):
-            def b2_column(pos):
-                return b2_f32[:, t * POSITIONS + pos : t * POSITIONS + pos + 1]
+        def multiply_unit(t, k):
+            if k < OFFSETS - 2:
+                for pos in range(POSITIONS):
+                    multiply(t, k, pos)
+            elif k == OFFSETS - 1:
+                for pos in range(POSITIONS):
+                    multiply(t, k - 1, pos)
+                    multiply(t, k, pos)
+                    pool_position(t, pos)
 
-            even = work.tile([P, 2, N], F32)
-            odd = work.tile([P, N], F32)
-            nc.scalar.activation(out=even[:, 0, :], in_=acc[0][:], func=RELU, bias=b2_column(0))
-            nc.vector.tensor_scalar(
-                out=odd[:], in0=acc[1][:], scalar1=b2_column(1), scalar2=None, op0=ADD
-            )
-            nc.scalar.activation(out=even[:, 1, :], in_=acc[2][:], func=RELU, bias=b2_column(2))
-            nc.vector.scalar_tensor_tensor(
-                out=odd[:], in0=acc[3][:], scalar=b2_column(3), in1=odd[:], op0=ADD, op1=MAX
-            )
-            nc.vector.tensor_tensor(out=odd[:], in0=odd[:], in1=even[:, 0, :], op=MAX)
-            nc.vector.tensor_tensor(out=g_grouped[:, :, t], in0=odd[:], in1=even[:, 1, :], op=MAX)
+        fc_codes = keep.tile([P, F], U32, align_bytes=64)
+        fc_scales = keep.tile([P, F], U8, align_bytes=64)
+        bias = keep.tile([P, F], BF16)
+        fc_views = {}
+
+        def load_dense():
+            fc_tile = raw_tile()
+            fc_views["raw"] = fc_tile[:, 0 : PACK * F].rearrange("p (t f) -> p t f", t=PACK)
+            fc_views["grouped"] = fc_tile[:, PACK * F : 2 * PACK * F]
+            nc.sync.dma_start(out=fc_views["raw"], in_=fc1_w.rearrange("(m t) f -> m t f", t=PACK))
+            nc.sync.dma_start(out=bias[:], in_=fc1_b.partition_broadcast(P))
 
         weight_units = [(t, k) for t in range(O_TILES) for k in range(OFFSETS)]
-        rounds = [weight_units[u : u + RUN] for u in range(0, len(weight_units), RUN)]
-        for r in range(len(rounds) + 2):
-            if r < len(rounds):
-                for t, k in rounds[r]:
-                    group_weights(t, k)
-                    if k == OFFSETS - 1 and t + 2 < O_TILES:
-                        raw_weights[t + 2] = load_weights(t + 2)
-            if 1 <= r <= len(rounds):
-                for t, k in rounds[r - 1]:
-                    quantise_weights(t, k)
-            if r >= 2:
-                for t, k in rounds[r - 2]:
-                    multiply(t, k)
-                    if k == OFFSETS - 1:
-                        pool_positions(t)
-            if r == len(rounds) // 2:
-                nc.vector.tensor_copy(out=fc_grouped[:], in_=fc_raw[:].rearrange("p t f -> p f t"))
-                nc.vector.quantize_mx(
-                    out=fc_codes[:].bitcast(FP8X4),
-                    scales=fc_scales[:],
-                    in_=fc_grouped[:].rearrange("p f t -> p (f t)"),
+        count = len(weight_units)
+        transposes(*weight_units[0])
+        for step in range(count + 2):
+            if step + 1 < count and by_transposes(weight_units[step + 1][0]):
+                transposes(*weight_units[step + 1])
+            if step < count:
+                t, k = weight_units[step]
+                if by_transposes(t):
+                    copy_banks(t, k)
+                    if k == OFFSETS - 1 and t + 3 < O_TILES:
+                        raw_weights[t + 3] = load_weights(t + 3)
+                    if k >= EARLY_FROM:
+                        for j in range(2 * (k - EARLY_FROM), min(2 * (k - EARLY_FROM) + 2, OFFSETS)):
+                            regroup_half(t + 1, j, 0, False)
+                else:
+                    regroup_half(t, k, HALF, k % 3 == 1)
+                    if k == OFFSETS - 1 and t == 1:
+                        load_dense()
+            if step == count - 1:
+                nc.scalar.copy(
+                    out=fc_views["grouped"].rearrange("p (f t) -> p f t", t=PACK),
+                    in_=fc_views["raw"].rearrange("p t f -> p f t"),
                 )
+            if 1 <= step <= count:
+                quantise_weights(*weight_units[step - 1])
+            if step == count:
+                nc.vector.quantize_mx(out=fc_codes[:].bitcast(FP8X4), scales=fc_scales[:], in_=fc_views["grouped"])
+            if step >= 2:
+                multiply_unit(*weight_units[step - 2])
 
-        bias = keep.tile([P, F], BF16)
-        nc.sync.dma_start(out=bias[:], in_=fc1_b.partition_broadcast(P))
         g_codes = keep.tile([P, N], U32, align_bytes=64)
         g_scales = keep.tile([P, N], U8, align_bytes=64)
         nc.vector.quantize_mx(
@@ -249,7 +262,7 @@ def tile_locallyconnectednet_pa_t_kernel(tc, h_pool1, w2, b2, fc1_w, fc1_b, out)
                 start=True,
                 stop=True,
             )
-            summed = work.tile([P, F], F32)
+            summed = work.tile([P, F], F32, tag="pooled", name="summed")
             nc.vector.tensor_tensor(out=summed[:], in0=dense[:], in1=bias[:], op=ADD)
             result = work.tile([P, F], F32)
             nc.scalar.activation(out=result[:], in_=summed[:], func=RELU)

@@ -32,6 +32,10 @@ HALF = P // 2
 FLOPS = 2 * N * O * C * TAPS + 2 * N * O * F
 
 EARLY_FROM = 4
+H_ON_VECTOR = ((1, 3, 5, 7), (3,))
+BANK_ON_VECTOR = (0, 1, 2)
+LATE_ON_SCALAR = (1, 2, 4, 5, 7, 8)
+LAG = 3
 
 
 def copy_on(nc, on_scalar, out, in_):
@@ -41,9 +45,9 @@ def copy_on(nc, on_scalar, out, in_):
         nc.vector.tensor_copy(out=out, in_=in_)
 
 
-def transpose_pair(nc, banks, ident, rows, inner, w):
+def transpose_pair(nc, new_bank, ident, rows, inner, w):
     words = rows.bitcast(F32).rearrange("r (p t w) -> r p t w", t=PACK, w=inner // 2)
-    bank = banks.tile([P, PACK * P], F32, tag="bank")
+    bank = new_bank()
     for t in range(PACK):
         nc.tensor.transpose(bank[:, t * P : (t + 1) * P], words[:, :, t, w], ident[:])
     return bank[:].bitcast(BF16).rearrange("p (t r e) -> p e r t", t=PACK, e=2)
@@ -58,8 +62,12 @@ def tile_locallyconnectednet_pa_t_kernel(tc, h_pool1, w2, b2, fc1_w, fc1_b, out)
         codes = stack.enter_context(tc.tile_pool(name="codes", bufs=6))
         stage = stack.enter_context(tc.tile_pool(name="stage", bufs=4))
         work = stack.enter_context(tc.tile_pool(name="work", bufs=2))
+        results = stack.enter_context(tc.tile_pool(name="results", bufs=N_TILES))
         banks = stack.enter_context(tc.psum_pool(name="banks", bufs=4))
         sums = stack.enter_context(tc.psum_pool(name="sums", bufs=1))
+
+        def ring_bank():
+            return banks.tile([P, PACK * P], F32, tag="bank", name="bank")
 
         def raw_tile():
             return raws.tile([P, C * TAPS], BF16, tag="raw", align_bytes=64, name="raw")
@@ -104,21 +112,24 @@ def tile_locallyconnectednet_pa_t_kernel(tc, h_pool1, w2, b2, fc1_w, fc1_b, out)
 
         h_codes = keep.tile([P, PIXELS, N], U32, align_bytes=64)
         h_scales = keep.tile([P, PIXELS, N], U8, align_bytes=64)
-        h_grouped = {}
+        late_stage = keep.tile([P, OFFSETS, POSITIONS, P, PACK], BF16, align_bytes=64)
+        pair_stage = late_stage[:].rearrange("p k i m c -> p (k i m c)")[:, 0 : PIXELS * P * PACK * 2].rearrange(
+            "p (w e r t) -> p w e r t", w=PIXELS // 2, e=2, t=PACK
+        )
 
         def group_images(nt, w):
             rows = raw_images[nt // 2][:, (nt % 2) * C * PIXELS : (nt % 2 + 1) * C * PIXELS]
-            bank = transpose_pair(nc, banks, ident, rows, PIXELS, w)
-            h_grouped[nt, w] = stage.tile([P, 2, P, PACK], BF16, align_bytes=64, tag="grouped", name="h_grouped")
-            copy_on(nc, (nt * (PIXELS // 2) + w) % 3 != 2, h_grouped[nt, w][:], bank)
+            bank = transpose_pair(nc, ring_bank, ident, rows, PIXELS, w)
+            copy_on(nc, w not in H_ON_VECTOR[nt % 2], pair_stage[:, w, :, (nt % 2) * P : (nt % 2 + 1) * P, :], bank)
 
         def quantise_images(nt, w):
-            for e in range(2):
-                nc.vector.quantize_mx(
-                    out=h_codes[:, 2 * w + e, nt * P : (nt + 1) * P].bitcast(FP8X4),
-                    scales=h_scales[:, 2 * w + e, nt * P : (nt + 1) * P],
-                    in_=h_grouped[nt, w][:, e].rearrange("p r t -> p (r t)"),
-                )
+            if nt % 2 == 1:
+                for e in range(2):
+                    nc.vector.quantize_mx(
+                        out=h_codes[:, 2 * w + e, (nt - 1) * P : (nt + 1) * P].bitcast(FP8X4),
+                        scales=h_scales[:, 2 * w + e, (nt - 1) * P : (nt + 1) * P],
+                        in_=pair_stage[:, w, e].rearrange("p r t -> p (r t)"),
+                    )
 
         image_units = [(nt, w) for nt in range(N_TILES) for w in range(PIXELS // 2)]
         for step in range(len(image_units) + 1):
@@ -130,7 +141,6 @@ def tile_locallyconnectednet_pa_t_kernel(tc, h_pool1, w2, b2, fc1_w, fc1_b, out)
             if step >= 1:
                 quantise_images(*image_units[step - 1])
 
-        late_stage = keep.tile([P, OFFSETS, POSITIONS, P, PACK], BF16, align_bytes=64)
         bank_views = {}
         w_grouped = {}
         w_codes = {}
@@ -141,14 +151,14 @@ def tile_locallyconnectednet_pa_t_kernel(tc, h_pool1, w2, b2, fc1_w, fc1_b, out)
 
         def transposes(t, k):
             bank_views[t, k] = [
-                transpose_pair(nc, banks, ident, raw_weights[t][:], TAPS, 2 * k + half) for half in range(2)
+                transpose_pair(nc, ring_bank, ident, raw_weights[t][:], TAPS, 2 * k + half) for half in range(2)
             ]
 
         def copy_banks(t, k):
             grouped = stage.tile([P, POSITIONS, P, PACK], BF16, align_bytes=64, tag="grouped", name="w_grouped")
             w_grouped[t, k] = grouped[:].rearrange("p i m c -> p (i m c)")
             copy_on(nc, True, grouped[:, 0:2], bank_views[t, k][0])
-            copy_on(nc, k >= EARLY_FROM, grouped[:, 2:4], bank_views[t, k][1])
+            copy_on(nc, k not in BANK_ON_VECTOR, grouped[:, 2:4], bank_views[t, k][1])
 
         def regroup_half(t, k, m0, on_scalar):
             taps = raw_weights[t][:].rearrange("p (m c q) -> p m c q", c=PACK, q=TAPS)
@@ -216,7 +226,7 @@ def tile_locallyconnectednet_pa_t_kernel(tc, h_pool1, w2, b2, fc1_w, fc1_b, out)
         weight_units = [(t, k) for t in range(O_TILES) for k in range(OFFSETS)]
         count = len(weight_units)
         transposes(*weight_units[0])
-        for step in range(count + 2):
+        for step in range(count + LAG):
             if step + 1 < count and by_transposes(weight_units[step + 1][0]):
                 transposes(*weight_units[step + 1])
             if step < count:
@@ -229,7 +239,7 @@ def tile_locallyconnectednet_pa_t_kernel(tc, h_pool1, w2, b2, fc1_w, fc1_b, out)
                         for j in range(2 * (k - EARLY_FROM), min(2 * (k - EARLY_FROM) + 2, OFFSETS)):
                             regroup_half(t + 1, j, 0, False)
                 else:
-                    regroup_half(t, k, HALF, k % 3 == 1)
+                    regroup_half(t, k, HALF, k in LATE_ON_SCALAR)
                     if k == OFFSETS - 1 and t == 1:
                         load_dense()
             if step == count - 1:
@@ -241,8 +251,8 @@ def tile_locallyconnectednet_pa_t_kernel(tc, h_pool1, w2, b2, fc1_w, fc1_b, out)
                 quantise_weights(*weight_units[step - 1])
             if step == count:
                 nc.vector.quantize_mx(out=fc_codes[:].bitcast(FP8X4), scales=fc_scales[:], in_=fc_views["grouped"])
-            if step >= 2:
-                multiply_unit(*weight_units[step - 2])
+            if step >= LAG:
+                multiply_unit(*weight_units[step - LAG])
 
         g_codes = keep.tile([P, N], U32, align_bytes=64)
         g_scales = keep.tile([P, N], U8, align_bytes=64)
@@ -264,6 +274,6 @@ def tile_locallyconnectednet_pa_t_kernel(tc, h_pool1, w2, b2, fc1_w, fc1_b, out)
             )
             summed = work.tile([P, F], F32, tag="pooled", name="summed")
             nc.vector.tensor_tensor(out=summed[:], in0=dense[:], in1=bias[:], op=ADD)
-            result = work.tile([P, F], F32)
+            result = results.tile([P, F], F32)
             nc.scalar.activation(out=result[:], in_=summed[:], func=RELU)
             nc.sync.dma_start(out=out[nt * P : (nt + 1) * P, :], in_=result[:])

@@ -33,9 +33,11 @@ FLOPS = 2 * N * O * C * TAPS + 2 * N * O * F
 
 EARLY_FROM = 4
 H_ON_VECTOR = ((1, 3, 5, 7), (3,))
-BANK_ON_VECTOR = (0, 1, 2)
+BANK_ON_VECTOR = (0, 1, 2, 3)
 LATE_ON_SCALAR = (1, 2, 4, 5, 7, 8)
-LAG = 3
+SUM_SETS = "yxxyx"
+TRANSPOSE_SETS = "x-y-"
+LAG = 4
 
 
 def copy_on(nc, on_scalar, out, in_):
@@ -59,15 +61,21 @@ def tile_locallyconnectednet_pa_t_kernel(tc, h_pool1, w2, b2, fc1_w, fc1_b, out)
         stack.enter_context(tc.manual_schedule())
         keep = stack.enter_context(tc.tile_pool(name="keep", bufs=1))
         raws = stack.enter_context(tc.tile_pool(name="raws", bufs=3))
-        codes = stack.enter_context(tc.tile_pool(name="codes", bufs=6))
+        codes = stack.enter_context(tc.tile_pool(name="codes", bufs=7))
         stage = stack.enter_context(tc.tile_pool(name="stage", bufs=4))
         work = stack.enter_context(tc.tile_pool(name="work", bufs=2))
-        results = stack.enter_context(tc.tile_pool(name="results", bufs=N_TILES))
-        banks = stack.enter_context(tc.psum_pool(name="banks", bufs=4))
-        sums = stack.enter_context(tc.psum_pool(name="sums", bufs=1))
+        psum = stack.enter_context(tc.psum_pool(name="psum", bufs=1))
+
+        ring = {"sets": "xy", "next": 0}
 
         def ring_bank():
-            return banks.tile([P, PACK * P], F32, tag="bank", name="bank")
+            ring["next"] = (ring["next"] + 1) % (POSITIONS * len(ring["sets"]))
+            return psum.tile(
+                [P, PACK * P], F32, name="%s%d" % (ring["sets"][ring["next"] // POSITIONS], ring["next"] % POSITIONS)
+            )
+
+        def sum_bank(user, pos):
+            return psum.tile([P, N], F32, name="%s%d" % (SUM_SETS[user], pos))
 
         def raw_tile():
             return raws.tile([P, C * TAPS], BF16, tag="raw", align_bytes=64, name="raw")
@@ -150,6 +158,7 @@ def tile_locallyconnectednet_pa_t_kernel(tc, h_pool1, w2, b2, fc1_w, fc1_b, out)
         g_grouped = keep.tile([P, N, PACK], BF16, align_bytes=64)
 
         def transposes(t, k):
+            ring["sets"] = TRANSPOSE_SETS[t]
             bank_views[t, k] = [
                 transpose_pair(nc, ring_bank, ident, raw_weights[t][:], TAPS, 2 * k + half) for half in range(2)
             ]
@@ -178,7 +187,7 @@ def tile_locallyconnectednet_pa_t_kernel(tc, h_pool1, w2, b2, fc1_w, fc1_b, out)
 
         def multiply(t, k, pos):
             if k == 0:
-                acc[pos] = sums.tile([P, N], F32, name="acc%d" % pos)
+                acc[pos] = sum_bank(t, pos)
             pixel = (pos // OUT_SIDE + k // WINDOW) * SIDE + pos % OUT_SIDE + k % WINDOW
             nc.tensor.matmul_mx(
                 out=acc[pos][:],
@@ -235,6 +244,10 @@ def tile_locallyconnectednet_pa_t_kernel(tc, h_pool1, w2, b2, fc1_w, fc1_b, out)
                     copy_banks(t, k)
                     if k == OFFSETS - 1 and t + 3 < O_TILES:
                         raw_weights[t + 3] = load_weights(t + 3)
+            if 1 <= step <= count:
+                quantise_weights(*weight_units[step - 1])
+            if step < count:
+                if by_transposes(t):
                     if k >= EARLY_FROM:
                         for j in range(2 * (k - EARLY_FROM), min(2 * (k - EARLY_FROM) + 2, OFFSETS)):
                             regroup_half(t + 1, j, 0, False)
@@ -247,8 +260,6 @@ def tile_locallyconnectednet_pa_t_kernel(tc, h_pool1, w2, b2, fc1_w, fc1_b, out)
                     out=fc_views["grouped"].rearrange("p (f t) -> p f t", t=PACK),
                     in_=fc_views["raw"].rearrange("p t f -> p f t"),
                 )
-            if 1 <= step <= count:
-                quantise_weights(*weight_units[step - 1])
             if step == count:
                 nc.vector.quantize_mx(out=fc_codes[:].bitcast(FP8X4), scales=fc_scales[:], in_=fc_views["grouped"])
             if step >= LAG:
@@ -262,7 +273,7 @@ def tile_locallyconnectednet_pa_t_kernel(tc, h_pool1, w2, b2, fc1_w, fc1_b, out)
             in_=g_grouped[:].rearrange("p n t -> p (n t)"),
         )
         for nt in range(N_TILES):
-            dense = sums.tile([P, F], F32, name="acc%d" % nt)
+            dense = sum_bank(O_TILES, nt)
             nc.tensor.matmul_mx(
                 out=dense[:],
                 lhsT=g_codes[:, nt * P : (nt + 1) * P].bitcast(FP8X4),
@@ -274,6 +285,6 @@ def tile_locallyconnectednet_pa_t_kernel(tc, h_pool1, w2, b2, fc1_w, fc1_b, out)
             )
             summed = work.tile([P, F], F32, tag="pooled", name="summed")
             nc.vector.tensor_tensor(out=summed[:], in0=dense[:], in1=bias[:], op=ADD)
-            result = results.tile([P, F], F32)
+            result = stage.tile([P, F], F32, align_bytes=64, tag="grouped", name="result")
             nc.scalar.activation(out=result[:], in_=summed[:], func=RELU)
             nc.sync.dma_start(out=out[nt * P : (nt + 1) * P, :], in_=result[:])

@@ -156,6 +156,8 @@ def tile_locallyconnectednet_pa_t_kernel(tc, h_pool1, w2, b2, fc1_w, fc1_b, out)
         acc = {}
         pooled = {}
         g_grouped = keep.tile([P, N, PACK], BF16, align_bytes=64)
+        g_codes = keep.tile([P, N], U32, align_bytes=64)
+        g_scales = keep.tile([P, N], U8, align_bytes=64)
 
         def transposes(t, k):
             ring["sets"] = TRANSPOSE_SETS[t]
@@ -204,6 +206,20 @@ def tile_locallyconnectednet_pa_t_kernel(tc, h_pool1, w2, b2, fc1_w, fc1_b, out)
             if pos == 0:
                 pooled[t] = work.tile([P, N], F32, tag="pooled", name="pooled")
                 nc.scalar.activation(out=pooled[t][:], in_=acc[0][:], func=RELU, bias=bias_column)
+            elif t == O_TILES - 1 and pos == POSITIONS - 1:
+                for piece in range(N_TILES + 1):
+                    if piece < N_TILES:
+                        cols = slice(piece * P, (piece + 1) * P)
+                        nc.vector.scalar_tensor_tensor(
+                            out=g_grouped[:, cols, t], in0=acc[pos][:, cols], scalar=bias_column, in1=pooled[t][:, cols], op0=ADD, op1=MAX
+                        )
+                    if piece >= 1:
+                        cols = slice((piece - 1) * P, piece * P)
+                        nc.vector.quantize_mx(
+                            out=g_codes[:, cols].bitcast(FP8X4),
+                            scales=g_scales[:, cols],
+                            in_=g_grouped[:, cols, :].rearrange("p n t -> p (n t)"),
+                        )
             else:
                 target = g_grouped[:, :, t] if pos == POSITIONS - 1 else pooled[t][:]
                 nc.vector.scalar_tensor_tensor(
@@ -265,13 +281,6 @@ def tile_locallyconnectednet_pa_t_kernel(tc, h_pool1, w2, b2, fc1_w, fc1_b, out)
             if step >= LAG:
                 multiply_unit(*weight_units[step - LAG])
 
-        g_codes = keep.tile([P, N], U32, align_bytes=64)
-        g_scales = keep.tile([P, N], U8, align_bytes=64)
-        nc.vector.quantize_mx(
-            out=g_codes[:].bitcast(FP8X4),
-            scales=g_scales[:],
-            in_=g_grouped[:].rearrange("p n t -> p (n t)"),
-        )
         for nt in range(N_TILES):
             dense = sum_bank(O_TILES, nt)
             nc.tensor.matmul_mx(
@@ -283,8 +292,7 @@ def tile_locallyconnectednet_pa_t_kernel(tc, h_pool1, w2, b2, fc1_w, fc1_b, out)
                 start=True,
                 stop=True,
             )
-            summed = work.tile([P, F], F32, tag="pooled", name="summed")
-            nc.vector.tensor_tensor(out=summed[:], in0=dense[:], in1=bias[:], op=ADD)
             result = stage.tile([P, F], F32, align_bytes=64, tag="grouped", name="result")
-            nc.scalar.activation(out=result[:], in_=summed[:], func=RELU)
+            nc.vector.tensor_tensor(out=result[:], in0=dense[:], in1=bias[:], op=ADD)
+            nc.scalar.activation(out=result[:], in_=result[:], func=RELU)
             nc.sync.dma_start(out=out[nt * P : (nt + 1) * P, :], in_=result[:])

@@ -221,10 +221,12 @@ def tile_locallyconnectednet_pa_t_kernel(tc, h_pool1, w2, b2, fc1_w, fc1_b, out)
                             in_=g_grouped[:, cols, :].rearrange("p n t -> p (n t)"),
                         )
             else:
-                target = g_grouped[:, :, t] if pos == POSITIONS - 1 else pooled[t][:]
                 nc.vector.scalar_tensor_tensor(
-                    out=target, in0=acc[pos][:], scalar=bias_column, in1=pooled[t][:], op0=ADD, op1=MAX
+                    out=pooled[t][:], in0=acc[pos][:], scalar=bias_column, in1=pooled[t][:], op0=ADD, op1=MAX
                 )
+
+        def round_pooled(t):
+            nc.scalar.copy(out=g_grouped[:, :, t], in_=pooled[t][:])
 
         def multiply_unit(t, k):
             if k < OFFSETS - 2:
@@ -278,6 +280,8 @@ def tile_locallyconnectednet_pa_t_kernel(tc, h_pool1, w2, b2, fc1_w, fc1_b, out)
                 )
             if step == count:
                 nc.vector.quantize_mx(out=fc_codes[:].bitcast(FP8X4), scales=fc_scales[:], in_=fc_views["grouped"])
+            if step >= LAG + 2 and weight_units[step - LAG - 2][1] == OFFSETS - 1:
+                round_pooled(weight_units[step - LAG - 2][0])
             if step >= LAG:
                 multiply_unit(*weight_units[step - LAG])
 

@@ -31,11 +31,14 @@ HALF = P // 2
 
 FLOPS = 2 * N * O * C * TAPS + 2 * N * O * F
 
+TAIL = (2, 2, 2, 4)
+RELU_V = (3,)
+BLAG = 1
 EARLY_FROM = 4
 H_ON_VECTOR = ((1, 3, 5, 7), (3,))
 BANK_ON_VECTOR = (0, 1, 2, 3)
 LATE_ON_SCALAR = (1, 2, 4, 5, 7, 8)
-SUM_SETS = "yxxyx"
+SUM_SETS = ("y", "x", "x", "yx", "y")
 TRANSPOSE_SETS = "x-y-"
 LAG = 4
 
@@ -61,7 +64,7 @@ def tile_locallyconnectednet_pa_t_kernel(tc, h_pool1, w2, b2, fc1_w, fc1_b, out)
         stack.enter_context(tc.manual_schedule())
         keep = stack.enter_context(tc.tile_pool(name="keep", bufs=1))
         raws = stack.enter_context(tc.tile_pool(name="raws", bufs=3))
-        codes = stack.enter_context(tc.tile_pool(name="codes", bufs=7))
+        codes = stack.enter_context(tc.tile_pool(name="codes", bufs=8))
         stage = stack.enter_context(tc.tile_pool(name="stage", bufs=4))
         work = stack.enter_context(tc.tile_pool(name="work", bufs=2))
         psum = stack.enter_context(tc.psum_pool(name="psum", bufs=1))
@@ -74,8 +77,10 @@ def tile_locallyconnectednet_pa_t_kernel(tc, h_pool1, w2, b2, fc1_w, fc1_b, out)
                 [P, PACK * P], F32, name="%s%d" % (ring["sets"][ring["next"] // POSITIONS], ring["next"] % POSITIONS)
             )
 
-        def sum_bank(user, pos):
-            return psum.tile([P, N], F32, name="%s%d" % (SUM_SETS[user], pos))
+        def sum_bank(user, pos, cols):
+            sets = SUM_SETS[user]
+            bank = psum.tile([P, N], F32, name="%s%d" % (sets[cols.start * len(sets) // N], pos))
+            return bank[:, 0 : cols.stop - cols.start]
 
         def raw_tile():
             return raws.tile([P, C * TAPS], BF16, tag="raw", align_bytes=64, name="raw")
@@ -155,7 +160,8 @@ def tile_locallyconnectednet_pa_t_kernel(tc, h_pool1, w2, b2, fc1_w, fc1_b, out)
         w_scales = {}
         acc = {}
         pooled = {}
-        g_grouped = keep.tile([P, N, PACK], BF16, align_bytes=64)
+        g_planar = keep.tile([P, PACK, N], BF16, align_bytes=64)
+        g_grouped = {}
         g_codes = keep.tile([P, N], U32, align_bytes=64)
         g_scales = keep.tile([P, N], U8, align_bytes=64)
 
@@ -187,56 +193,61 @@ def tile_locallyconnectednet_pa_t_kernel(tc, h_pool1, w2, b2, fc1_w, fc1_b, out)
             w_scales[t, k] = codes.tile([P, POSITIONS * P], U8, align_bytes=64, name="w_scales")
             nc.vector.quantize_mx(out=w_codes[t, k][:].bitcast(FP8X4), scales=w_scales[t, k][:], in_=w_grouped[t, k])
 
-        def multiply(t, k, pos):
+        def multiply(t, k, pos, cols):
             if k == 0:
-                acc[pos] = sum_bank(t, pos)
+                acc[pos, cols.start] = sum_bank(t, pos, cols)
             pixel = (pos // OUT_SIDE + k // WINDOW) * SIDE + pos % OUT_SIDE + k % WINDOW
             nc.tensor.matmul_mx(
-                out=acc[pos][:],
+                out=acc[pos, cols.start],
                 lhsT=w_codes[t, k][:, pos * P : (pos + 1) * P].bitcast(FP8X4),
                 lhsT_scale=w_scales[t, k][:, pos * P : (pos + 1) * P],
-                rhs=h_codes[:, pixel, :].bitcast(FP8X4),
-                rhs_scale=h_scales[:, pixel, :],
+                rhs=h_codes[:, pixel, cols].bitcast(FP8X4),
+                rhs_scale=h_scales[:, pixel, cols],
                 start=(k == 0),
                 stop=(k == OFFSETS - 1),
             )
 
-        def pool_position(t, pos):
+        def pool_position(t, pos, cols):
             bias_column = b2_f32[:, t * POSITIONS + pos : t * POSITIONS + pos + 1]
+            bank = acc[pos, cols.start]
             if pos == 0:
-                pooled[t] = work.tile([P, N], F32, tag="pooled", name="pooled")
-                nc.scalar.activation(out=pooled[t][:], in_=acc[0][:], func=RELU, bias=bias_column)
-            elif t == O_TILES - 1 and pos == POSITIONS - 1:
-                for piece in range(N_TILES + 1):
-                    if piece < N_TILES:
-                        cols = slice(piece * P, (piece + 1) * P)
-                        nc.vector.scalar_tensor_tensor(
-                            out=g_grouped[:, cols, t], in0=acc[pos][:, cols], scalar=bias_column, in1=pooled[t][:, cols], op0=ADD, op1=MAX
-                        )
-                    if piece >= 1:
-                        cols = slice((piece - 1) * P, piece * P)
-                        nc.vector.quantize_mx(
-                            out=g_codes[:, cols].bitcast(FP8X4),
-                            scales=g_scales[:, cols],
-                            in_=g_grouped[:, cols, :].rearrange("p n t -> p (n t)"),
-                        )
-            else:
+                if cols.start == 0:
+                    pooled[t] = work.tile([P, N], F32, tag="pooled", name="pooled")
+                nc.scalar.activation(out=pooled[t][:, cols], in_=bank, func=RELU, bias=bias_column)
+            elif pos < POSITIONS - 1 or t < O_TILES - 1:
                 nc.vector.scalar_tensor_tensor(
-                    out=pooled[t][:], in0=acc[pos][:], scalar=bias_column, in1=pooled[t][:], op0=ADD, op1=MAX
+                    out=g_planar[:, t, cols] if pos == POSITIONS - 1 else pooled[t][:, cols], in0=bank, scalar=bias_column, in1=pooled[t][:, cols], op0=ADD, op1=MAX
                 )
+            else:
+                pieces = [slice(c, c + P) for c in range(cols.start, cols.stop, P)]
+                for i, here in enumerate(pieces):
+                    nc.vector.scalar_tensor_tensor(
+                        out=g_planar[:, t, here], in0=bank[:, i * P : (i + 1) * P], scalar=bias_column, in1=pooled[t][:, here], op0=ADD, op1=MAX
+                    )
+                for i in range(len(pieces) + 1):
+                    if i < len(pieces):
+                        here = pieces[i]
+                        g_grouped[here.start] = stage.tile([P, P, PACK], BF16, align_bytes=64, tag="grouped", name="g_grouped")
+                        nc.vector.tensor_copy(out=g_grouped[here.start][:], in_=g_planar[:, :, here].rearrange("p t n -> p n t"))
+                    if i >= 1:
+                        here = pieces[i - 1]
+                        nc.vector.quantize_mx(
+                            out=g_codes[:, here].bitcast(FP8X4),
+                            scales=g_scales[:, here],
+                            in_=g_grouped[here.start][:].rearrange("p n t -> p (n t)"),
+                        )
 
-        def round_pooled(t):
-            nc.scalar.copy(out=g_grouped[:, :, t], in_=pooled[t][:])
-
-        def multiply_unit(t, k):
-            if k < OFFSETS - 2:
-                for pos in range(POSITIONS):
-                    multiply(t, k, pos)
+        def multiply_unit(t, k, halves):
+            if k < OFFSETS - TAIL[t]:
+                for cols in halves:
+                    for pos in range(POSITIONS):
+                        multiply(t, k, pos, cols)
             elif k == OFFSETS - 1:
-                for pos in range(POSITIONS):
-                    multiply(t, k - 1, pos)
-                    multiply(t, k, pos)
-                    pool_position(t, pos)
+                for cols in halves:
+                    for pos in range(POSITIONS):
+                        for kk in range(OFFSETS - TAIL[t], OFFSETS):
+                            multiply(t, kk, pos, cols)
+                        pool_position(t, pos, cols)
 
         fc_codes = keep.tile([P, F], U32, align_bytes=64)
         fc_scales = keep.tile([P, F], U8, align_bytes=64)
@@ -253,7 +264,7 @@ def tile_locallyconnectednet_pa_t_kernel(tc, h_pool1, w2, b2, fc1_w, fc1_b, out)
         weight_units = [(t, k) for t in range(O_TILES) for k in range(OFFSETS)]
         count = len(weight_units)
         transposes(*weight_units[0])
-        for step in range(count + LAG):
+        for step in range(count + LAG + BLAG):
             if step + 1 < count and by_transposes(weight_units[step + 1][0]):
                 transposes(*weight_units[step + 1])
             if step < count:
@@ -280,15 +291,19 @@ def tile_locallyconnectednet_pa_t_kernel(tc, h_pool1, w2, b2, fc1_w, fc1_b, out)
                 )
             if step == count:
                 nc.vector.quantize_mx(out=fc_codes[:].bitcast(FP8X4), scales=fc_scales[:], in_=fc_views["grouped"])
-            if step >= LAG + 2 and weight_units[step - LAG - 2][1] == OFFSETS - 1:
-                round_pooled(weight_units[step - LAG - 2][0])
             if step >= LAG:
-                multiply_unit(*weight_units[step - LAG])
+                t, k = weight_units[step - LAG] if step - LAG < count else (O_TILES, 0)
+                if t < O_TILES - 1:
+                    multiply_unit(t, k, [slice(0, N)])
+                elif t < O_TILES:
+                    multiply_unit(t, k, [slice(0, N // 2)])
+                if step - LAG - BLAG >= 0 and weight_units[step - LAG - BLAG][0] == O_TILES - 1:
+                    multiply_unit(*weight_units[step - LAG - BLAG], [slice(N // 2, N)])
 
         for nt in range(N_TILES):
-            dense = sum_bank(O_TILES, nt)
+            dense = sum_bank(O_TILES, nt, slice(0, N))
             nc.tensor.matmul_mx(
-                out=dense[:],
+                out=dense,
                 lhsT=g_codes[:, nt * P : (nt + 1) * P].bitcast(FP8X4),
                 lhsT_scale=g_scales[:, nt * P : (nt + 1) * P],
                 rhs=fc_codes[:].bitcast(FP8X4),
@@ -297,6 +312,9 @@ def tile_locallyconnectednet_pa_t_kernel(tc, h_pool1, w2, b2, fc1_w, fc1_b, out)
                 stop=True,
             )
             result = stage.tile([P, F], F32, align_bytes=64, tag="grouped", name="result")
-            nc.vector.tensor_tensor(out=result[:], in0=dense[:], in1=bias[:], op=ADD)
-            nc.scalar.activation(out=result[:], in_=result[:], func=RELU)
+            nc.vector.tensor_tensor(out=result[:], in0=dense, in1=bias[:], op=ADD)
+            if nt in RELU_V:
+                nc.vector.tensor_scalar(out=result[:], in0=result[:], scalar1=0.0, scalar2=None, op0=MAX)
+            else:
+                nc.scalar.activation(out=result[:], in_=result[:], func=RELU)
             nc.sync.dma_start(out=out[nt * P : (nt + 1) * P, :], in_=result[:])

@@ -27,32 +27,37 @@ O = 512
 F = 512
 N_TILES = N // P
 O_TILES = O // P
-HALF = P // 2
+LAST = O_TILES - 1
+UNIT = POSITIONS * P
 
 FLOPS = 2 * N * O * C * TAPS + 2 * N * O * F
 
-TAIL = (2, 2, 2, 4)
-RELU_V = (3,)
-BLAG = 1
-EARLY_FROM = 4
-H_ON_VECTOR = ((1, 3, 5, 7), (3,))
-BANK_ON_VECTOR = (0, 1, 2, 3)
-LATE_ON_SCALAR = (1, 2, 4, 5, 7, 8)
-SUM_SETS = ("y", "x", "x", "yx", "y")
-TRANSPOSE_SETS = "x-y-"
-LAG = 4
+BY_TRANSPOSES = (True, True, False, False)
+
+IMAGE_ON_VECTOR = ((1, 3, 5, 7), (3, 7), (1, 3, 5, 7), (3,))
+BANK_ON_VECTOR = (tuple(range(2, 2 * OFFSETS, 3)), tuple(range(1, 2 * OFFSETS, 6)))
+FIRST_PIECE = {2: P // 2, 3: 5 * P // 8}
+FIRST_ON_VECTOR = {2: tuple(range(OFFSETS)), 3: tuple(range(0, OFFSETS, 2))}
+SECOND_ON_VECTOR = {2: tuple(range(1, OFFSETS, 3)), 3: (0, 4)}
+AHEAD = {2: 8, 3: 4}
+AHEAD_RATE = {2: 1, 3: 4}
+PAUSE = 3
+
+SUM_SETS = ("y", "y", "x", "yx")
+LAG = (5, 6, 4, 5)
+POOL_LAG = (1, 3, 1)
+TAIL = (3, 3, 3, 4)
 
 
-def copy_on(nc, on_scalar, out, in_):
-    if on_scalar:
-        nc.scalar.copy(out=out, in_=in_)
-    else:
+def copy_on(nc, on_vector, out, in_):
+    if on_vector:
         nc.vector.tensor_copy(out=out, in_=in_)
+    else:
+        nc.scalar.copy(out=out, in_=in_)
 
 
-def transpose_pair(nc, new_bank, ident, rows, inner, w):
+def transpose_pair(nc, bank, ident, rows, inner, w):
     words = rows.bitcast(F32).rearrange("r (p t w) -> r p t w", t=PACK, w=inner // 2)
-    bank = new_bank()
     for t in range(PACK):
         nc.tensor.transpose(bank[:, t * P : (t + 1) * P], words[:, :, t, w], ident[:])
     return bank[:].bitcast(BF16).rearrange("p (t r e) -> p e r t", t=PACK, e=2)
@@ -64,23 +69,17 @@ def tile_locallyconnectednet_pa_t_kernel(tc, h_pool1, w2, b2, fc1_w, fc1_b, out)
         stack.enter_context(tc.manual_schedule())
         keep = stack.enter_context(tc.tile_pool(name="keep", bufs=1))
         raws = stack.enter_context(tc.tile_pool(name="raws", bufs=3))
-        codes = stack.enter_context(tc.tile_pool(name="codes", bufs=8))
+        codes = stack.enter_context(tc.tile_pool(name="codes", bufs=10))
         stage = stack.enter_context(tc.tile_pool(name="stage", bufs=4))
-        work = stack.enter_context(tc.tile_pool(name="work", bufs=2))
+        work = stack.enter_context(tc.tile_pool(name="work", bufs=1))
         psum = stack.enter_context(tc.psum_pool(name="psum", bufs=1))
 
-        ring = {"sets": "xy", "next": 0}
+        ring = {"next": 0}
 
-        def ring_bank():
-            ring["next"] = (ring["next"] + 1) % (POSITIONS * len(ring["sets"]))
-            return psum.tile(
-                [P, PACK * P], F32, name="%s%d" % (ring["sets"][ring["next"] // POSITIONS], ring["next"] % POSITIONS)
-            )
-
-        def sum_bank(user, pos, cols):
-            sets = SUM_SETS[user]
-            bank = psum.tile([P, N], F32, name="%s%d" % (sets[cols.start * len(sets) // N], pos))
-            return bank[:, 0 : cols.stop - cols.start]
+        def ring_bank(sets):
+            ring["next"] = (ring["next"] + 1) % (POSITIONS * len(sets))
+            name = "%s%d" % (sets[ring["next"] // POSITIONS], ring["next"] % POSITIONS)
+            return psum.tile([P, PACK * P], F32, name=name)
 
         def raw_tile():
             return raws.tile([P, C * TAPS], BF16, tag="raw", align_bytes=64, name="raw")
@@ -95,12 +94,9 @@ def tile_locallyconnectednet_pa_t_kernel(tc, h_pool1, w2, b2, fc1_w, fc1_b, out)
                 )
             return raw
 
-        def by_transposes(t):
-            return t % 2 == 0
-
         def load_weights(t):
             raw = raw_tile()
-            if by_transposes(t):
+            if BY_TRANSPOSES[t]:
                 source = w2.rearrange("(m t) c k i j -> t m (c k i j)", t=O_TILES)[t]
                 cut = C * TAPS // 2
                 for x0 in (0, cut):
@@ -108,8 +104,8 @@ def tile_locallyconnectednet_pa_t_kernel(tc, h_pool1, w2, b2, fc1_w, fc1_b, out)
             else:
                 source = w2.rearrange("(m t) (p c) k i j -> t p m (c k i j)", t=O_TILES, c=PACK)[t]
                 target = raw[:].rearrange("p (m x) -> p m x", m=P)
-                for m0 in (0, HALF):
-                    nc.sync.dma_start(out=target[:, m0 : m0 + HALF, :], in_=source[:, m0 : m0 + HALF, :])
+                for piece in (slice(0, FIRST_PIECE[t]), slice(FIRST_PIECE[t], P)):
+                    nc.sync.dma_start(out=target[:, piece, :], in_=source[:, piece, :])
             return raw
 
         raw_images = [load_images(0), load_images(1)]
@@ -125,196 +121,224 @@ def tile_locallyconnectednet_pa_t_kernel(tc, h_pool1, w2, b2, fc1_w, fc1_b, out)
 
         h_codes = keep.tile([P, PIXELS, N], U32, align_bytes=64)
         h_scales = keep.tile([P, PIXELS, N], U8, align_bytes=64)
-        late_stage = keep.tile([P, OFFSETS, POSITIONS, P, PACK], BF16, align_bytes=64)
-        pair_stage = late_stage[:].rearrange("p k i m c -> p (k i m c)")[:, 0 : PIXELS * P * PACK * 2].rearrange(
-            "p (w e r t) -> p w e r t", w=PIXELS // 2, e=2, t=PACK
-        )
-
-        def group_images(nt, w):
-            rows = raw_images[nt // 2][:, (nt % 2) * C * PIXELS : (nt % 2 + 1) * C * PIXELS]
-            bank = transpose_pair(nc, ring_bank, ident, rows, PIXELS, w)
-            copy_on(nc, w not in H_ON_VECTOR[nt % 2], pair_stage[:, w, :, (nt % 2) * P : (nt % 2 + 1) * P, :], bank)
-
-        def quantise_images(nt, w):
-            if nt % 2 == 1:
-                for e in range(2):
-                    nc.vector.quantize_mx(
-                        out=h_codes[:, 2 * w + e, (nt - 1) * P : (nt + 1) * P].bitcast(FP8X4),
-                        scales=h_scales[:, 2 * w + e, (nt - 1) * P : (nt + 1) * P],
-                        in_=pair_stage[:, w, e].rearrange("p r t -> p (r t)"),
-                    )
-
-        image_units = [(nt, w) for nt in range(N_TILES) for w in range(PIXELS // 2)]
-        for step in range(len(image_units) + 1):
-            if step < len(image_units):
-                group_images(*image_units[step])
-                if (step + 1) % (2 * PIXELS // 2) == 0:
-                    pair = step // (2 * PIXELS // 2)
-                    raw_weights[pair + 1] = load_weights(pair + 1)
-            if step >= 1:
-                quantise_images(*image_units[step - 1])
-
-        bank_views = {}
-        w_grouped = {}
-        w_codes = {}
-        w_scales = {}
-        acc = {}
-        pooled = {}
         g_planar = keep.tile([P, PACK, N], BF16, align_bytes=64)
-        g_grouped = {}
+        bias = keep.tile([P, F], BF16)
+        fc_codes = keep.tile([P, F], U32, align_bytes=64)
+        fc_scales = keep.tile([P, F], U8, align_bytes=64)
         g_codes = keep.tile([P, N], U32, align_bytes=64)
         g_scales = keep.tile([P, N], U8, align_bytes=64)
+        waiting = keep.tile([P, OFFSETS, UNIT * PACK], BF16, align_bytes=64)
 
-        def transposes(t, k):
-            ring["sets"] = TRANSPOSE_SETS[t]
-            bank_views[t, k] = [
-                transpose_pair(nc, ring_bank, ident, raw_weights[t][:], TAPS, 2 * k + half) for half in range(2)
-            ]
+        banks = {}
+        grouped = {}
+        w_codes = {}
+        w_scales = {}
+        sums = {}
+        pooled = {}
+        g_grouped = {}
 
-        def copy_banks(t, k):
-            grouped = stage.tile([P, POSITIONS, P, PACK], BF16, align_bytes=64, tag="grouped", name="w_grouped")
-            w_grouped[t, k] = grouped[:].rearrange("p i m c -> p (i m c)")
-            copy_on(nc, True, grouped[:, 0:2], bank_views[t, k][0])
-            copy_on(nc, k not in BANK_ON_VECTOR, grouped[:, 2:4], bank_views[t, k][1])
+        def grouped_tile():
+            return stage.tile([P, UNIT * PACK], BF16, tag="grouped", align_bytes=64, name="grouped")[:]
 
-        def regroup_half(t, k, m0, on_scalar):
-            taps = raw_weights[t][:].rearrange("p (m c q) -> p m c q", c=PACK, q=TAPS)
-            copy_on(
-                nc,
-                on_scalar,
-                late_stage[:, k, :, m0 : m0 + HALF, :].rearrange("p i m c -> p m c i"),
-                taps[:, m0 : m0 + HALF, :, k * POSITIONS : (k + 1) * POSITIONS],
-            )
+        def transposes(unit):
+            kind, tile, index = unit
+            if kind == "image":
+                rows = raw_images[tile // 2][:, (tile % 2) * C * PIXELS : (tile % 2 + 1) * C * PIXELS]
+                banks[unit] = [transpose_pair(nc, ring_bank("xy"), ident, rows, PIXELS, index)]
+            elif kind == "long":
+                rows = raw_weights[tile][:]
+                banks[unit] = [transpose_pair(nc, ring_bank("x"), ident, rows, TAPS, 2 * index + h) for h in range(2)]
 
-        def quantise_weights(t, k):
-            if not by_transposes(t):
-                w_grouped[t, k] = late_stage[:, k].rearrange("p i m c -> p (i m c)")
-            w_codes[t, k] = codes.tile([P, POSITIONS * P], U32, align_bytes=64, name="w_codes")
-            w_scales[t, k] = codes.tile([P, POSITIONS * P], U8, align_bytes=64, name="w_scales")
-            nc.vector.quantize_mx(out=w_codes[t, k][:].bitcast(FP8X4), scales=w_scales[t, k][:], in_=w_grouped[t, k])
+        def empty_banks(unit):
+            kind, tile, index = unit
+            if kind == "image":
+                target = waiting[:, index].rearrange("p (e n t) -> p e n t", e=2, t=PACK)
+                cols = slice((tile % 2) * P, (tile % 2 + 1) * P)
+                copy_on(nc, index in IMAGE_ON_VECTOR[tile], target[:, :, cols, :], banks[unit][0])
+            elif kind == "long":
+                grouped[unit] = grouped_tile()
+                target = grouped[unit].rearrange("p (i m c) -> p i m c", i=POSITIONS, c=PACK)
+                for h in range(2):
+                    on_vector = 2 * index + h in BANK_ON_VECTOR[tile]
+                    copy_on(nc, on_vector, target[:, 2 * h : 2 * h + 2], banks[unit][h])
 
-        def multiply(t, k, pos, cols):
+        def regroup(tile, k, piece, on_vector):
+            taps = raw_weights[tile][:].rearrange("p (m c q) -> p m c q", c=PACK, q=TAPS)
+            target = waiting[:, k].rearrange("p (i m c) -> p m c i", i=POSITIONS, c=PACK)
+            copy_on(nc, on_vector, target[:, piece], taps[:, piece, :, k * POSITIONS : (k + 1) * POSITIONS])
+
+        def quantise(unit):
+            kind, tile, index = unit
+            if kind == "image" and tile % 2 == 1:
+                cols = slice((tile - 1) * P, (tile + 1) * P)
+                source = waiting[:, index].rearrange("p (e x) -> p e x", e=2)
+                for e in range(2):
+                    nc.vector.quantize_mx(
+                        out=h_codes[:, 2 * index + e, cols].bitcast(FP8X4),
+                        scales=h_scales[:, 2 * index + e, cols],
+                        in_=source[:, e],
+                    )
+            elif kind in ("long", "short"):
+                w_codes[tile, index] = codes.tile([P, UNIT], U32, align_bytes=64, name="w_codes")
+                w_scales[tile, index] = codes.tile([P, UNIT], U8, align_bytes=64, name="w_scales")
+                nc.vector.quantize_mx(
+                    out=w_codes[tile, index][:].bitcast(FP8X4),
+                    scales=w_scales[tile, index][:],
+                    in_=grouped[unit] if kind == "long" else waiting[:, index],
+                )
+
+        def multiply(tile, k, pos, cols, sum_set):
             if k == 0:
-                acc[pos, cols.start] = sum_bank(t, pos, cols)
+                bank = psum.tile([P, N], F32, name="%s%d" % (sum_set, pos))
+                sums[tile, pos, cols.start] = bank[:, 0 : cols.stop - cols.start]
             pixel = (pos // OUT_SIDE + k // WINDOW) * SIDE + pos % OUT_SIDE + k % WINDOW
             nc.tensor.matmul_mx(
-                out=acc[pos, cols.start],
-                lhsT=w_codes[t, k][:, pos * P : (pos + 1) * P].bitcast(FP8X4),
-                lhsT_scale=w_scales[t, k][:, pos * P : (pos + 1) * P],
+                out=sums[tile, pos, cols.start],
+                lhsT=w_codes[tile, k][:, pos * P : (pos + 1) * P].bitcast(FP8X4),
+                lhsT_scale=w_scales[tile, k][:, pos * P : (pos + 1) * P],
                 rhs=h_codes[:, pixel, cols].bitcast(FP8X4),
                 rhs_scale=h_scales[:, pixel, cols],
                 start=(k == 0),
                 stop=(k == OFFSETS - 1),
             )
 
-        def pool_position(t, pos, cols):
-            bias_column = b2_f32[:, t * POSITIONS + pos : t * POSITIONS + pos + 1]
-            bank = acc[pos, cols.start]
+        def multiply_offset(tile, k, cols, sum_set):
+            if k < OFFSETS - TAIL[tile]:
+                for pos in range(POSITIONS):
+                    multiply(tile, k, pos, cols, sum_set)
+            elif k == OFFSETS - 1:
+                for pos in range(POSITIONS):
+                    for kk in range(OFFSETS - TAIL[tile], OFFSETS):
+                        multiply(tile, kk, pos, cols, sum_set)
+                    if tile == LAST:
+                        pool(tile, pos, cols)
+
+        def pool(tile, pos, cols):
+            bank = sums[tile, pos, cols.start]
+            bias_column = b2_f32[:, tile * POSITIONS + pos : tile * POSITIONS + pos + 1]
             if pos == 0:
                 if cols.start == 0:
-                    pooled[t] = work.tile([P, N], F32, tag="pooled", name="pooled")
-                nc.scalar.activation(out=pooled[t][:, cols], in_=bank, func=RELU, bias=bias_column)
-            elif pos < POSITIONS - 1 or t < O_TILES - 1:
+                    pooled[tile] = work.tile([P, N], F32, tag="pooled", name="pooled")
+                nc.scalar.activation(out=pooled[tile][:, cols], in_=bank, func=RELU, bias=bias_column)
+            elif pos < POSITIONS - 1 or tile < LAST:
+                target = g_planar[:, tile, cols] if pos == POSITIONS - 1 else pooled[tile][:, cols]
                 nc.vector.scalar_tensor_tensor(
-                    out=g_planar[:, t, cols] if pos == POSITIONS - 1 else pooled[t][:, cols], in0=bank, scalar=bias_column, in1=pooled[t][:, cols], op0=ADD, op1=MAX
+                    out=target, in0=bank, scalar=bias_column, in1=pooled[tile][:, cols], op0=ADD, op1=MAX
                 )
             else:
-                pieces = [slice(c, c + P) for c in range(cols.start, cols.stop, P)]
-                for i, here in enumerate(pieces):
-                    nc.vector.scalar_tensor_tensor(
-                        out=g_planar[:, t, here], in0=bank[:, i * P : (i + 1) * P], scalar=bias_column, in1=pooled[t][:, here], op0=ADD, op1=MAX
-                    )
-                for i in range(len(pieces) + 1):
-                    if i < len(pieces):
-                        here = pieces[i]
-                        g_grouped[here.start] = stage.tile([P, P, PACK], BF16, align_bytes=64, tag="grouped", name="g_grouped")
-                        nc.vector.tensor_copy(out=g_grouped[here.start][:], in_=g_planar[:, :, here].rearrange("p t n -> p n t"))
-                    if i >= 1:
-                        here = pieces[i - 1]
-                        nc.vector.quantize_mx(
-                            out=g_codes[:, here].bitcast(FP8X4),
-                            scales=g_scales[:, here],
-                            in_=g_grouped[here.start][:].rearrange("p n t -> p (n t)"),
-                        )
+                finish_g(tile, bank, bias_column, cols)
 
-        def multiply_unit(t, k, halves):
-            if k < OFFSETS - TAIL[t]:
-                for cols in halves:
-                    for pos in range(POSITIONS):
-                        multiply(t, k, pos, cols)
-            elif k == OFFSETS - 1:
-                for cols in halves:
-                    for pos in range(POSITIONS):
-                        for kk in range(OFFSETS - TAIL[t], OFFSETS):
-                            multiply(t, kk, pos, cols)
-                        pool_position(t, pos, cols)
+        def finish_g(tile, bank, bias_column, cols):
+            pieces = [slice(n0, n0 + P) for n0 in range(cols.start, cols.stop, P)]
+            for piece in pieces:
+                nc.vector.scalar_tensor_tensor(
+                    out=g_planar[:, tile, piece],
+                    in0=bank[:, piece.start - cols.start : piece.stop - cols.start],
+                    scalar=bias_column,
+                    in1=pooled[tile][:, piece],
+                    op0=ADD,
+                    op1=MAX,
+                )
+            for piece in pieces:
+                g_grouped[piece.start] = stage.tile([P, P, PACK], BF16, tag="grouped", align_bytes=64, name="g_grouped")
+                nc.vector.tensor_copy(
+                    out=g_grouped[piece.start][:], in_=g_planar[:, :, piece].rearrange("p t n -> p n t")
+                )
+            for piece in pieces:
+                nc.vector.quantize_mx(
+                    out=g_codes[:, piece].bitcast(FP8X4),
+                    scales=g_scales[:, piece],
+                    in_=g_grouped[piece.start][:].rearrange("p n t -> p (n t)"),
+                )
 
-        fc_codes = keep.tile([P, F], U32, align_bytes=64)
-        fc_scales = keep.tile([P, F], U8, align_bytes=64)
-        bias = keep.tile([P, F], BF16)
-        fc_views = {}
+        units = [("image", nt, w) for nt in range(N_TILES) for w in range(PIXELS // 2)]
+        starts = []
+        for t in range(O_TILES):
+            if t == LAST:
+                units += [("pause", t, i) for i in range(PAUSE)]
+            starts.append(len(units))
+            units += [("long" if BY_TRANSPOSES[t] else "short", t, k) for k in range(OFFSETS)]
+        count = len(units)
+        everyone = slice(0, N)
+        halves = (slice(0, N // 2), slice(N // 2, N))
 
-        def load_dense():
-            fc_tile = raw_tile()
-            fc_views["raw"] = fc_tile[:, 0 : PACK * F].rearrange("p (t f) -> p t f", t=PACK)
-            fc_views["grouped"] = fc_tile[:, PACK * F : 2 * PACK * F]
-            nc.sync.dma_start(out=fc_views["raw"], in_=fc1_w.rearrange("(m t) f -> m t f", t=PACK))
-            nc.sync.dma_start(out=bias[:], in_=fc1_b.partition_broadcast(P))
+        pool_at = {starts[t] + OFFSETS - 1 + LAG[t] + POOL_LAG[t]: t for t in range(LAST)}
+        ahead_at = {}
+        for t in AHEAD:
+            for k in range(OFFSETS):
+                ahead_at.setdefault(starts[t] - AHEAD[t] + k // AHEAD_RATE[t], []).append((t, k))
 
-        weight_units = [(t, k) for t in range(O_TILES) for k in range(OFFSETS)]
-        count = len(weight_units)
-        transposes(*weight_units[0])
-        for step in range(count + LAG + BLAG):
-            if step + 1 < count and by_transposes(weight_units[step + 1][0]):
-                transposes(*weight_units[step + 1])
+        transposes(units[0])
+        for step in range(count + LAG[LAST]):
+            if step + 1 < count:
+                transposes(units[step + 1])
+            pooling = pool_at.get(step)
+            if pooling is not None:
+                pool(pooling, 0, everyone)
+                pool(pooling, 1, everyone)
             if step < count:
-                t, k = weight_units[step]
-                if by_transposes(t):
-                    copy_banks(t, k)
-                    if k == OFFSETS - 1 and t + 3 < O_TILES:
-                        raw_weights[t + 3] = load_weights(t + 3)
+                kind, tile, index = units[step]
+                empty_banks(units[step])
+                if units[step] == ("image", 1, PIXELS // 2 - 1):
+                    raw_weights[1] = load_weights(1)
+                if units[step] == ("image", 3, PIXELS // 2 - 1):
+                    raw_weights[2] = load_weights(2)
+                if units[step] == ("long", 0, OFFSETS - 1):
+                    raw_weights[3] = load_weights(3)
+                if units[step] == ("long", 1, OFFSETS - 1):
+                    fc_tile = raw_tile()
+                    fc_raw = fc_tile[:, 0 : PACK * F].rearrange("p (t f) -> p t f", t=PACK)
+                    fc_grouped = fc_tile[:, PACK * F : 2 * PACK * F]
+                    nc.sync.dma_start(out=fc_raw, in_=fc1_w.rearrange("(m t) f -> m t f", t=PACK))
+                    nc.sync.dma_start(out=bias[:], in_=fc1_b.partition_broadcast(P))
             if 1 <= step <= count:
-                quantise_weights(*weight_units[step - 1])
-            if step < count:
-                if by_transposes(t):
-                    if k >= EARLY_FROM:
-                        for j in range(2 * (k - EARLY_FROM), min(2 * (k - EARLY_FROM) + 2, OFFSETS)):
-                            regroup_half(t + 1, j, 0, False)
-                else:
-                    regroup_half(t, k, HALF, k in LATE_ON_SCALAR)
-                    if k == OFFSETS - 1 and t == 1:
-                        load_dense()
+                quantise(units[step - 1])
+            if pooling is not None:
+                pool(pooling, 2, everyone)
+            for t, k in ahead_at.get(step, []):
+                regroup(t, k, slice(0, FIRST_PIECE[t]), k in FIRST_ON_VECTOR[t])
+            if step < count and kind == "short":
+                regroup(tile, index, slice(FIRST_PIECE[tile], P), index in SECOND_ON_VECTOR[tile])
+            if pooling is not None:
+                pool(pooling, 3, everyone)
             if step == count - 1:
                 nc.scalar.copy(
-                    out=fc_views["grouped"].rearrange("p (f t) -> p f t", t=PACK),
-                    in_=fc_views["raw"].rearrange("p t f -> p f t"),
+                    out=fc_grouped.rearrange("p (f t) -> p f t", t=PACK), in_=fc_raw.rearrange("p t f -> p f t")
                 )
-            if step == count:
-                nc.vector.quantize_mx(out=fc_codes[:].bitcast(FP8X4), scales=fc_scales[:], in_=fc_views["grouped"])
-            if step >= LAG:
-                t, k = weight_units[step - LAG] if step - LAG < count else (O_TILES, 0)
-                if t < O_TILES - 1:
-                    multiply_unit(t, k, [slice(0, N)])
-                elif t < O_TILES:
-                    multiply_unit(t, k, [slice(0, N // 2)])
-                if step - LAG - BLAG >= 0 and weight_units[step - LAG - BLAG][0] == O_TILES - 1:
-                    multiply_unit(*weight_units[step - LAG - BLAG], [slice(N // 2, N)])
+            if step == count + 1:
+                nc.vector.quantize_mx(out=fc_codes[:].bitcast(FP8X4), scales=fc_scales[:], in_=fc_grouped)
+            for t in range(O_TILES):
+                k = step - LAG[t] - starts[t]
+                if 0 <= k < OFFSETS:
+                    if t < LAST:
+                        multiply_offset(t, k, everyone, SUM_SETS[t])
+                    else:
+                        for half in range(2):
+                            multiply_offset(t, k, halves[half], SUM_SETS[t][half])
 
         for nt in range(N_TILES):
-            dense = sum_bank(O_TILES, nt, slice(0, N))
+            rows = slice(nt * P, (nt + 1) * P)
+            bank = psum.tile([P, F], F32, name="y%d" % nt)
             nc.tensor.matmul_mx(
-                out=dense,
-                lhsT=g_codes[:, nt * P : (nt + 1) * P].bitcast(FP8X4),
-                lhsT_scale=g_scales[:, nt * P : (nt + 1) * P],
+                out=bank[:],
+                lhsT=g_codes[:, rows].bitcast(FP8X4),
+                lhsT_scale=g_scales[:, rows],
                 rhs=fc_codes[:].bitcast(FP8X4),
                 rhs_scale=fc_scales[:],
                 start=True,
                 stop=True,
             )
-            result = stage.tile([P, F], F32, align_bytes=64, tag="grouped", name="result")
-            nc.vector.tensor_tensor(out=result[:], in0=dense, in1=bias[:], op=ADD)
-            if nt in RELU_V:
-                nc.vector.tensor_scalar(out=result[:], in0=result[:], scalar1=0.0, scalar2=None, op0=MAX)
+            result = waiting[:, nt, 0 : 2 * F].bitcast(F32)
+            if nt < N_TILES - 1:
+                nc.vector.tensor_tensor(out=result, in0=bank[:], in1=bias[:], op=ADD)
+                nc.scalar.activation(out=result, in_=result, func=RELU)
+                nc.sync.dma_start(out=out[rows, :], in_=result)
             else:
-                nc.scalar.activation(out=result[:], in_=result[:], func=RELU)
-            nc.sync.dma_start(out=out[nt * P : (nt + 1) * P, :], in_=result[:])
+                parts = (slice(0, F // 2), slice(F // 2, F))
+                for part in parts:
+                    nc.vector.tensor_tensor(out=result[:, part], in0=bank[:, part], in1=bias[:, part], op=ADD)
+                for part in parts:
+                    nc.vector.tensor_scalar(
+                        out=result[:, part], in0=result[:, part], scalar1=0.0, scalar2=None, op0=MAX
+                    )
+                    nc.sync.dma_start(out=out[rows, part], in_=result[:, part])

from contextlib import ExitStack

import concourse.mybir as mybir
from concourse.masks import make_identity

F32 = mybir.dt.float32
BF16 = mybir.dt.bfloat16
U32 = mybir.dt.uint32
U8 = mybir.dt.uint8
FP8X4 = mybir.dt.float8_e4m3fn_x4
ADD = mybir.AluOpType.add
MAX = mybir.AluOpType.max
RELU = mybir.ActivationFunctionType.Relu

P = 128
PACK = 4
N = 512
C = 512
SIDE = 4
PIXELS = SIDE * SIDE
WINDOW = 3
OFFSETS = WINDOW * WINDOW
OUT_SIDE = 2
POSITIONS = OUT_SIDE * OUT_SIDE
TAPS = OFFSETS * POSITIONS
O = 512
F = 512
N_TILES = N // P
O_TILES = O // P
LAST = O_TILES - 1
UNIT = POSITIONS * P

FLOPS = 2 * N * O * C * TAPS + 2 * N * O * F

BY_TRANSPOSES = (True, True, False, False)

IMAGE_ON_VECTOR = ((1, 3, 5, 7), (3, 7), (1, 3, 5, 7), (3,))
BANK_ON_VECTOR = (tuple(range(2, 2 * OFFSETS, 3)), tuple(range(1, 2 * OFFSETS, 6)))
FIRST_PIECE = {2: P // 2, 3: 5 * P // 8}
FIRST_ON_VECTOR = {2: tuple(range(OFFSETS)), 3: tuple(range(0, OFFSETS, 2))}
SECOND_ON_VECTOR = {2: tuple(range(1, OFFSETS, 3)), 3: (0, 4)}
AHEAD = {2: 8, 3: 4}
AHEAD_RATE = {2: 1, 3: 4}
PAUSE = 3

SUM_SETS = ("y", "y", "x", "yx")
LAG = (5, 6, 4, 5)
POOL_LAG = (1, 3, 1)
TAIL = (3, 3, 3, 4)


def copy_on(nc, on_vector, out, in_):
    if on_vector:
        nc.vector.tensor_copy(out=out, in_=in_)
    else:
        nc.scalar.copy(out=out, in_=in_)


def transpose_pair(nc, bank, ident, rows, inner, w):
    words = rows.bitcast(F32).rearrange("r (p t w) -> r p t w", t=PACK, w=inner // 2)
    for t in range(PACK):
        nc.tensor.transpose(bank[:, t * P : (t + 1) * P], words[:, :, t, w], ident[:])
    return bank[:].bitcast(BF16).rearrange("p (t r e) -> p e r t", t=PACK, e=2)


def tile_locallyconnectednet_pa_t_kernel(tc, h_pool1, w2, b2, fc1_w, fc1_b, out):
    nc = tc.nc
    with ExitStack() as stack:
        stack.enter_context(tc.manual_schedule())
        keep = stack.enter_context(tc.tile_pool(name="keep", bufs=1))
        raws = stack.enter_context(tc.tile_pool(name="raws", bufs=3))
        codes = stack.enter_context(tc.tile_pool(name="codes", bufs=10))
        stage = stack.enter_context(tc.tile_pool(name="stage", bufs=4))
        work = stack.enter_context(tc.tile_pool(name="work", bufs=1))
        psum = stack.enter_context(tc.psum_pool(name="psum", bufs=1))

        ring = {"next": 0}

        def ring_bank(sets):
            ring["next"] = (ring["next"] + 1) % (POSITIONS * len(sets))
            name = "%s%d" % (sets[ring["next"] // POSITIONS], ring["next"] % POSITIONS)
            return psum.tile([P, PACK * P], F32, name=name)

        def raw_tile():
            return raws.tile([P, C * TAPS], BF16, tag="raw", align_bytes=64, name="raw")

        def load_images(pair):
            raw = raw_tile()
            for half in range(2):
                nt = 2 * pair + half
                nc.sync.dma_start(
                    out=raw[:, half * C * PIXELS : (half + 1) * C * PIXELS],
                    in_=h_pool1[nt * P : (nt + 1) * P].rearrange("n c y x -> n (c y x)"),
                )
            return raw

        def load_weights(t):
            raw = raw_tile()
            if BY_TRANSPOSES[t]:
                source = w2.rearrange("(m t) c k i j -> t m (c k i j)", t=O_TILES)[t]
                cut = C * TAPS // 2
                for x0 in (0, cut):
                    nc.sync.dma_start(out=raw[:, x0 : x0 + cut], in_=source[:, x0 : x0 + cut])
            else:
                source = w2.rearrange("(m t) (p c) k i j -> t p m (c k i j)", t=O_TILES, c=PACK)[t]
                target = raw[:].rearrange("p (m x) -> p m x", m=P)
                for piece in (slice(0, FIRST_PIECE[t]), slice(FIRST_PIECE[t], P)):
                    nc.sync.dma_start(out=target[:, piece, :], in_=source[:, piece, :])
            return raw

        raw_images = [load_images(0), load_images(1)]
        raw_weights = {0: load_weights(0)}

        ident = keep.tile([P, P], F32)
        make_identity(nc, ident[:])

        b2_bf = keep.tile([P, O_TILES * POSITIONS], BF16)
        nc.scalar.dma_start(out=b2_bf[:], in_=b2.rearrange("(m t) i j -> m (t i j)", t=O_TILES))
        b2_f32 = keep.tile([P, O_TILES * POSITIONS], F32)
        nc.vector.tensor_copy(out=b2_f32[:], in_=b2_bf[:])

        h_codes = keep.tile([P, PIXELS, N], U32, align_bytes=64)
        h_scales = keep.tile([P, PIXELS, N], U8, align_bytes=64)
        g_planar = keep.tile([P, PACK, N], BF16, align_bytes=64)
        bias = keep.tile([P, F], BF16)
        fc_codes = keep.tile([P, F], U32, align_bytes=64)
        fc_scales = keep.tile([P, F], U8, align_bytes=64)
        g_codes = keep.tile([P, N], U32, align_bytes=64)
        g_scales = keep.tile([P, N], U8, align_bytes=64)
        waiting = keep.tile([P, OFFSETS, UNIT * PACK], BF16, align_bytes=64)

        banks = {}
        grouped = {}
        w_codes = {}
        w_scales = {}
        sums = {}
        pooled = {}
        g_grouped = {}

        def grouped_tile():
            return stage.tile([P, UNIT * PACK], BF16, tag="grouped", align_bytes=64, name="grouped")[:]

        def transposes(unit):
            kind, tile, index = unit
            if kind == "image":
                rows = raw_images[tile // 2][:, (tile % 2) * C * PIXELS : (tile % 2 + 1) * C * PIXELS]
                banks[unit] = [transpose_pair(nc, ring_bank("xy"), ident, rows, PIXELS, index)]
            elif kind == "long":
                rows = raw_weights[tile][:]
                banks[unit] = [transpose_pair(nc, ring_bank("x"), ident, rows, TAPS, 2 * index + h) for h in range(2)]

        def empty_banks(unit):
            kind, tile, index = unit
            if kind == "image":
                target = waiting[:, index].rearrange("p (e n t) -> p e n t", e=2, t=PACK)
                cols = slice((tile % 2) * P, (tile % 2 + 1) * P)
                copy_on(nc, index in IMAGE_ON_VECTOR[tile], target[:, :, cols, :], banks[unit][0])
            elif kind == "long":
                grouped[unit] = grouped_tile()
                target = grouped[unit].rearrange("p (i m c) -> p i m c", i=POSITIONS, c=PACK)
                for h in range(2):
                    on_vector = 2 * index + h in BANK_ON_VECTOR[tile]
                    copy_on(nc, on_vector, target[:, 2 * h : 2 * h + 2], banks[unit][h])

        def regroup(tile, k, piece, on_vector):
            taps = raw_weights[tile][:].rearrange("p (m c q) -> p m c q", c=PACK, q=TAPS)
            target = waiting[:, k].rearrange("p (i m c) -> p m c i", i=POSITIONS, c=PACK)
            copy_on(nc, on_vector, target[:, piece], taps[:, piece, :, k * POSITIONS : (k + 1) * POSITIONS])

        def quantise(unit):
            kind, tile, index = unit
            if kind == "image" and tile % 2 == 1:
                cols = slice((tile - 1) * P, (tile + 1) * P)
                source = waiting[:, index].rearrange("p (e x) -> p e x", e=2)
                for e in range(2):
                    nc.vector.quantize_mx(
                        out=h_codes[:, 2 * index + e, cols].bitcast(FP8X4),
                        scales=h_scales[:, 2 * index + e, cols],
                        in_=source[:, e],
                    )
            elif kind in ("long", "short"):
                w_codes[tile, index] = codes.tile([P, UNIT], U32, align_bytes=64, name="w_codes")
                w_scales[tile, index] = codes.tile([P, UNIT], U8, align_bytes=64, name="w_scales")
                nc.vector.quantize_mx(
                    out=w_codes[tile, index][:].bitcast(FP8X4),
                    scales=w_scales[tile, index][:],
                    in_=grouped[unit] if kind == "long" else waiting[:, index],
                )

        def multiply(tile, k, pos, cols, sum_set):
            if k == 0:
                bank = psum.tile([P, N], F32, name="%s%d" % (sum_set, pos))
                sums[tile, pos, cols.start] = bank[:, 0 : cols.stop - cols.start]
            pixel = (pos // OUT_SIDE + k // WINDOW) * SIDE + pos % OUT_SIDE + k % WINDOW
            nc.tensor.matmul_mx(
                out=sums[tile, pos, cols.start],
                lhsT=w_codes[tile, k][:, pos * P : (pos + 1) * P].bitcast(FP8X4),
                lhsT_scale=w_scales[tile, k][:, pos * P : (pos + 1) * P],
                rhs=h_codes[:, pixel, cols].bitcast(FP8X4),
                rhs_scale=h_scales[:, pixel, cols],
                start=(k == 0),
                stop=(k == OFFSETS - 1),
            )

        def multiply_offset(tile, k, cols, sum_set):
            if k < OFFSETS - TAIL[tile]:
                for pos in range(POSITIONS):
                    multiply(tile, k, pos, cols, sum_set)
            elif k == OFFSETS - 1:
                for pos in range(POSITIONS):
                    for kk in range(OFFSETS - TAIL[tile], OFFSETS):
                        multiply(tile, kk, pos, cols, sum_set)
                    if tile == LAST:
                        pool(tile, pos, cols)

        def pool(tile, pos, cols):
            bank = sums[tile, pos, cols.start]
            bias_column = b2_f32[:, tile * POSITIONS + pos : tile * POSITIONS + pos + 1]
            if pos == 0:
                if cols.start == 0:
                    pooled[tile] = work.tile([P, N], F32, tag="pooled", name="pooled")
                nc.scalar.activation(out=pooled[tile][:, cols], in_=bank, func=RELU, bias=bias_column)
            elif pos < POSITIONS - 1 or tile < LAST:
                target = g_planar[:, tile, cols] if pos == POSITIONS - 1 else pooled[tile][:, cols]
                nc.vector.scalar_tensor_tensor(
                    out=target, in0=bank, scalar=bias_column, in1=pooled[tile][:, cols], op0=ADD, op1=MAX
                )
            else:
                finish_g(tile, bank, bias_column, cols)

        def finish_g(tile, bank, bias_column, cols):
            pieces = [slice(n0, n0 + P) for n0 in range(cols.start, cols.stop, P)]
            for piece in pieces:
                nc.vector.scalar_tensor_tensor(
                    out=g_planar[:, tile, piece],
                    in0=bank[:, piece.start - cols.start : piece.stop - cols.start],
                    scalar=bias_column,
                    in1=pooled[tile][:, piece],
                    op0=ADD,
                    op1=MAX,
                )
            for piece in pieces:
                g_grouped[piece.start] = stage.tile([P, P, PACK], BF16, tag="grouped", align_bytes=64, name="g_grouped")
                nc.vector.tensor_copy(
                    out=g_grouped[piece.start][:], in_=g_planar[:, :, piece].rearrange("p t n -> p n t")
                )
            for piece in pieces:
                nc.vector.quantize_mx(
                    out=g_codes[:, piece].bitcast(FP8X4),
                    scales=g_scales[:, piece],
                    in_=g_grouped[piece.start][:].rearrange("p n t -> p (n t)"),
                )

        units = [("image", nt, w) for nt in range(N_TILES) for w in range(PIXELS // 2)]
        starts = []
        for t in range(O_TILES):
            if t == LAST:
                units += [("pause", t, i) for i in range(PAUSE)]
            starts.append(len(units))
            units += [("long" if BY_TRANSPOSES[t] else "short", t, k) for k in range(OFFSETS)]
        count = len(units)
        everyone = slice(0, N)
        halves = (slice(0, N // 2), slice(N // 2, N))

        pool_at = {starts[t] + OFFSETS - 1 + LAG[t] + POOL_LAG[t]: t for t in range(LAST)}
        ahead_at = {}
        for t in AHEAD:
            for k in range(OFFSETS):
                ahead_at.setdefault(starts[t] - AHEAD[t] + k // AHEAD_RATE[t], []).append((t, k))

        transposes(units[0])
        for step in range(count + LAG[LAST]):
            if step + 1 < count:
                transposes(units[step + 1])
            pooling = pool_at.get(step)
            if pooling is not None:
                pool(pooling, 0, everyone)
                pool(pooling, 1, everyone)
            if step < count:
                kind, tile, index = units[step]
                empty_banks(units[step])
                if units[step] == ("image", 1, PIXELS // 2 - 1):
                    raw_weights[1] = load_weights(1)
                if units[step] == ("image", 3, PIXELS // 2 - 1):
                    raw_weights[2] = load_weights(2)
                if units[step] == ("long", 0, OFFSETS - 1):
                    raw_weights[3] = load_weights(3)
                if units[step] == ("long", 1, OFFSETS - 1):
                    fc_tile = raw_tile()
                    fc_raw = fc_tile[:, 0 : PACK * F].rearrange("p (t f) -> p t f", t=PACK)
                    fc_grouped = fc_tile[:, PACK * F : 2 * PACK * F]
                    nc.sync.dma_start(out=fc_raw, in_=fc1_w.rearrange("(m t) f -> m t f", t=PACK))
                    nc.sync.dma_start(out=bias[:], in_=fc1_b.partition_broadcast(P))
            if 1 <= step <= count:
                quantise(units[step - 1])
            if pooling is not None:
                pool(pooling, 2, everyone)
            for t, k in ahead_at.get(step, []):
                regroup(t, k, slice(0, FIRST_PIECE[t]), k in FIRST_ON_VECTOR[t])
            if step < count and kind == "short":
                regroup(tile, index, slice(FIRST_PIECE[tile], P), index in SECOND_ON_VECTOR[tile])
            if pooling is not None:
                pool(pooling, 3, everyone)
            if step == count - 1:
                nc.scalar.copy(
                    out=fc_grouped.rearrange("p (f t) -> p f t", t=PACK), in_=fc_raw.rearrange("p t f -> p f t")
                )
            if step == count + 1:
                nc.vector.quantize_mx(out=fc_codes[:].bitcast(FP8X4), scales=fc_scales[:], in_=fc_grouped)
            for t in range(O_TILES):
                k = step - LAG[t] - starts[t]
                if 0 <= k < OFFSETS:
                    if t < LAST:
                        multiply_offset(t, k, everyone, SUM_SETS[t])
                    else:
                        for half in range(2):
                            multiply_offset(t, k, halves[half], SUM_SETS[t][half])

        for nt in range(N_TILES):
            rows = slice(nt * P, (nt + 1) * P)
            bank = psum.tile([P, F], F32, name="y%d" % nt)
            nc.tensor.matmul_mx(
                out=bank[:],
                lhsT=g_codes[:, rows].bitcast(FP8X4),
                lhsT_scale=g_scales[:, rows],
                rhs=fc_codes[:].bitcast(FP8X4),
                rhs_scale=fc_scales[:],
                start=True,
                stop=True,
            )
            result = waiting[:, nt, 0 : 2 * F].bitcast(F32)
            if nt < N_TILES - 1:
                nc.vector.tensor_tensor(out=result, in0=bank[:], in1=bias[:], op=ADD)
                nc.scalar.activation(out=result, in_=result, func=RELU)
                nc.sync.dma_start(out=out[rows, :], in_=result)
            else:
                parts = (slice(0, F // 2), slice(F // 2, F))
                for part in parts:
                    nc.vector.tensor_tensor(out=result[:, part], in0=bank[:, part], in1=bias[:, part], op=ADD)
                for part in parts:
                    nc.vector.tensor_scalar(
                        out=result[:, part], in0=result[:, part], scalar1=0.0, scalar2=None, op0=MAX
                    )
                    nc.sync.dma_start(out=out[rows, part], in_=result[:, part])
